import numpy as np
import ml_dtypes


def mxq(x, axis, fmt="e4m3"):
    dtype, down = {"e4m3": (ml_dtypes.float8_e4m3fn, 7), "e5m2": (ml_dtypes.float8_e5m2, 14)}[fmt]
    v = np.moveaxis(np.asarray(x, np.float32).astype(ml_dtypes.bfloat16).astype(np.float64), axis, -1)
    blocks = v.reshape(v.shape[:-1] + (-1, 32))
    amax = np.abs(blocks).max(-1, keepdims=True)
    byte = np.maximum(np.where(amax > 0, np.frexp(amax)[1] - 1 + 127, 0) - down, 1)
    scale = np.exp2(byte - 127.0)
    codes = (blocks / scale).astype(np.float32).astype(dtype).astype(np.float64)
    return np.moveaxis((codes * scale).reshape(v.shape), -1, axis)


WIDE = False


def mx_kscale(k):
    if not WIDE:
        return np.ones(k)
    levels = np.array([10, -10, 5, -5, 0])
    a = np.random.permutation(np.resize(levels, k // 512 * 4)).reshape(k // 512, 4)
    idx = np.arange(k)
    return np.exp2(a[idx // 512, idx % 128 // 32])


BF16 = ml_dtypes.bfloat16


def bf(x):
    return np.asarray(x, np.float32).astype(BF16)


def f64(x):
    return np.asarray(x).astype(np.float64)


B, S, DV, DL, D = 2, 512, 1024, 1024, 1024
EPS = 1e-5
SIGMA = 1.7


def layernorm(x, g, b):
    m = x.mean(-1, keepdims=True)
    v = np.square(x - m).mean(-1, keepdims=True)
    return (x - m) / np.sqrt(v + EPS) * g + b


def setup_inputs():
    t = mx_kscale(D + D)
    z = SIGMA * np.random.standard_normal((B, S, S))
    e = np.exp(z - z.max(-1, keepdims=True))
    return {
        'A': bf(e / e.sum(-1, keepdims=True)),
        'vp': bf(np.maximum(np.random.standard_normal((B, S, D)), 0.0) * t[:D]),
        'lp': bf(np.maximum(np.random.standard_normal((B, S, D)), 0.0) * t[D:]),
        'oW': bf(np.random.standard_normal((D + D, D)) / np.sqrt(D + D) / t[:, None]),
        'ob': bf(0.1 * np.random.standard_normal(D)),
        'og': bf(1.0 + 0.1 * np.random.standard_normal(D)),
        'obeta': bf(0.1 * np.random.standard_normal(D)),
    }


def reference(A, vp, lp, oW, ob, og, obeta):
    a = f64(A)
    aligned_vision = mxq(a, 2, 'e4m3') @ mxq(f64(vp), 1, 'e4m3')
    aligned_language = mxq(a, 1, 'e4m3').transpose(0, 2, 1) @ mxq(f64(lp), 1, 'e4m3')
    combined = np.concatenate([aligned_vision, aligned_language], axis=-1)
    h = (mxq(combined, 2, 'e4m3') @ mxq(f64(oW), 0, 'e4m3')) + f64(ob)
    return np.maximum(layernorm(h, f64(og), f64(obeta)), 0.0)

@@ -1,0 +1,253 @@
+from contextlib import ExitStack
+
+import concourse.mybir as mybir
+from concourse.masks import make_identity
+
+F32 = mybir.dt.float32
+BF16 = mybir.dt.bfloat16
+U32 = mybir.dt.uint32
+U8 = mybir.dt.uint8
+FP8X4 = mybir.dt.float8_e4m3fn_x4
+ALU = mybir.AluOpType
+ACT = mybir.ActivationFunctionType
+
+P = 128
+B, S, D = 2, 512, 1024
+EPS = 1e-5
+FLOPS = 2 * (2 * B * S * S * D) + 2 * (B * S) * (2 * D) * D
+
+SPLIT2 = ("v", "s")
+
+
+def tile_clawmatrix_pb_kernel(tc, A, vp, lp, oW, ob, og, obeta, out):
+    nc = tc.nc
+    with ExitStack() as ctx:
+        raw = ctx.enter_context(tc.tile_pool(name="raw", bufs=1))
+        grp = ctx.enter_context(tc.tile_pool(name="grp", bufs=6))
+        keep = ctx.enter_context(tc.tile_pool(name="keep", bufs=1))
+        cbp = ctx.enter_context(tc.tile_pool(name="cbp", bufs=4))
+        hp = ctx.enter_context(tc.tile_pool(name="hp", bufs=8))
+        up = ctx.enter_context(tc.tile_pool(name="up", bufs=3))
+        sm = ctx.enter_context(tc.tile_pool(name="sm", bufs=8))
+        ps1 = ctx.enter_context(tc.psum_pool(name="ps1", bufs=4))
+        ps2 = ctx.enter_context(tc.psum_pool(name="ps2", bufs=4))
+
+        eps_t = keep.tile([P, 1], F32, name="eps_t")
+        nc.vector.memset(eps_t[:], EPS)
+        warm = keep.tile([P, 1], F32, name="warm")
+        nc.scalar.activation(out=warm[:], in_=eps_t[:], func=ACT.Sqrt)
+        ident = keep.tile([P, P], F32, name="ident")
+        make_identity(nc, ident[:])
+
+        A_sb, vp_sb, lp_sb = [], [], []
+
+        def load_batch(b):
+            a = raw.tile([P, 4, S], BF16, name="A_sb%d" % b)
+            nc.sync.dma_start(out=a[:], in_=A[b].rearrange("(t p) j -> p t j", p=P))
+            v = raw.tile([P, 4, D], BF16, name="vp_sb%d" % b)
+            for u in range(2):
+                nc.sync.dma_start(
+                    out=v[:, 2 * u : 2 * u + 2, :],
+                    in_=vp[b, 256 * u : 256 * u + 256, :].rearrange("(q e) d -> q e d", e=2),
+                )
+            l = raw.tile([P, 4, D], BF16, name="lp_sb%d" % b)
+            nc.sync.dma_start(out=l[:], in_=lp[b].rearrange("(t p) d -> p t d", p=P))
+            A_sb.append(a)
+            vp_sb.append(v)
+            lp_sb.append(l)
+
+        load_batch(0)
+        oW_v = oW.rearrange("(g t p) n -> g p t n", t=4, p=P)
+        oW_sb = []
+        for g in range(4):
+            w = raw.tile([P, 4, D], BF16, name="oW_sb%d" % g)
+            nc.sync.dma_start(out=w[:], in_=oW_v[g])
+            oW_sb.append(w)
+        ob_b = keep.tile([P, D], BF16, name="ob_b")
+        nc.sync.dma_start(out=ob_b[:], in_=ob.partition_broadcast(P))
+        load_batch(1)
+        og_b = keep.tile([P, D], BF16, name="og_b")
+        nc.sync.dma_start(out=og_b[:], in_=og.partition_broadcast(P))
+        be_b = keep.tile([P, D], BF16, name="be_b")
+        nc.sync.dma_start(out=be_b[:], in_=obeta.partition_broadcast(P))
+
+        def regroup(eng, src):
+            g = grp.tile([P, 512, 4], BF16, name="g", tag="grp", align_bytes=64)
+            d4 = g[:].rearrange("p (c i) t -> p c t i", i=4)
+            s4 = src.rearrange("p t (c i) -> p c t i", i=4)
+            if eng == "v":
+                nc.vector.tensor_copy(out=d4, in_=s4)
+            else:
+                nc.scalar.copy(out=d4, in_=s4)
+            return g
+
+        def quantise(g, codes, scales):
+            nc.vector.quantize_mx(
+                out=codes.bitcast(FP8X4),
+                scales=scales,
+                in_=g,
+            )
+
+        def kfirst(src, width, codes, scales, engs):
+            gs = []
+            for c in range(width // 512):
+                gs.append(regroup(engs[c % len(engs)], src[:, :, 512 * c : 512 * c + 512]))
+            for c in range(width // 512):
+                quantise(
+                    gs[c][:].rearrange("p w t -> p (w t)"),
+                    codes[:, 512 * c : 512 * c + 512],
+                    scales[:, 512 * c : 512 * c + 512],
+                )
+
+        AT_c, AT_s, A_c, A_s, vp_c, vp_s, lp_c, lp_s = [], [], [], [], [], [], [], []
+
+        def prep(b):
+            atc = keep.tile([P, S], U32, name="AT_c%d" % b, align_bytes=64)
+            ats = keep.tile([P, S], U8, name="AT_s%d" % b, align_bytes=64)
+            ac = keep.tile([P, S], U32, name="A_c%d" % b, align_bytes=64)
+            as_ = keep.tile([P, S], U8, name="A_s%d" % b, align_bytes=64)
+            vc = keep.tile([P, D], U32, name="vp_c%d" % b, align_bytes=64)
+            vs = keep.tile([P, D], U8, name="vp_s%d" % b, align_bytes=64)
+            lc = keep.tile([P, D], U32, name="lp_c%d" % b, align_bytes=64)
+            ls = keep.tile([P, D], U8, name="lp_s%d" % b, align_bytes=64)
+            gt = grp.tile([P, 512, 4], BF16, name="gt", tag="grp", align_bytes=64)
+            g32 = gt[:].rearrange("p w t -> p (w t)").bitcast(F32).rearrange("p (i u) -> p i u", u=2)
+            for half in range(2):
+                xt = ps1.tile([P, 2, 256], F32, name="xt", tag="s1")
+                for u in range(2):
+                    for hh in range(2):
+                        it = 2 * half + hh
+                        nc.tensor.transpose(
+                            xt[:, u, 128 * hh : 128 * hh + 128],
+                            A_sb[b][:, it, :].bitcast(F32)[:, 128 * u : 128 * u + 128],
+                            ident[:],
+                        )
+                nc.scalar.copy(
+                    out=g32[:, 256 * half : 256 * half + 256, :],
+                    in_=xt[:].rearrange("p u i -> p i u"),
+                )
+            ga = regroup("v", A_sb[b][:, :, :])
+            quantise(ga[:].rearrange("p w t -> p (w t)"), ac[:], as_[:])
+            quantise(gt[:].rearrange("p w t -> p (w t)"), atc[:], ats[:])
+            kfirst(vp_sb[b], D, vc, vs, SPLIT2)
+            kfirst(lp_sb[b], D, lc, ls, SPLIT2)
+            AT_c.append(atc)
+            AT_s.append(ats)
+            A_c.append(ac)
+            A_s.append(as_)
+            vp_c.append(vc)
+            vp_s.append(vs)
+            lp_c.append(lc)
+            lp_s.append(ls)
+
+        oW_c = keep.tile([P, 4, D], U32, name="oW_c", align_bytes=64)
+        oW_s = keep.tile([P, 4, D], U8, name="oW_s", align_bytes=64)
+
+        def prep_oW(g):
+            kfirst(oW_sb[g], D, oW_c[:, g, :], oW_s[:, g, :], SPLIT2)
+
+        cb = {}
+
+        def stage1(tau):
+            b, sg = divmod(tau, 4)
+            cols = slice(128 * sg, 128 * sg + 128)
+            cbg = grp.tile([P, 4, 128, 4], BF16, name="cbg", tag="grp", align_bytes=64)
+            for g in range(4):
+                if g < 2:
+                    wc, ws, rc, rs = vp_c[b], vp_s[b], AT_c[b], AT_s[b]
+                else:
+                    wc, ws, rc, rs = lp_c[b], lp_s[b], A_c[b], A_s[b]
+                bank = ps1.tile([P, 4, 128], F32, name="bank", tag="s1")
+                for t in range(4):
+                    c0 = 128 * (4 * (g % 2) + t)
+                    nc.tensor.matmul_mx(
+                        out=bank[:, t, :],
+                        lhsT=wc[:, c0 : c0 + 128].bitcast(FP8X4),
+                        lhsT_scale=ws[:, c0 : c0 + 128],
+                        rhs=rc[:, cols].bitcast(FP8X4),
+                        rhs_scale=rs[:, cols],
+                        start=True,
+                        stop=True,
+                    )
+                nc.scalar.copy(out=cbg[:, g, :, :], in_=bank[:].rearrange("p t s -> p s t"))
+            cc = cbp.tile([P, 512], U32, name="cb_c", tag="cb_c", align_bytes=64)
+            cs = cbp.tile([P, 512], U8, name="cb_s", tag="cb_s", align_bytes=64)
+            quantise(cbg[:].rearrange("p g s t -> p (g s t)"), cc[:], cs[:])
+            cb[tau] = (cc, cs)
+
+        hs = {}
+
+        def stage2(tau):
+            cc, cs = cb[tau]
+            h = hp.tile([P, D], F32, name="h", tag="h")
+            sums = sm.tile([P, 2], F32, name="sums", tag="sums")
+            for nh in range(2):
+                acc = ps2.tile([P, 512], F32, name="acc", tag="s2")
+                ncols = slice(512 * nh, 512 * nh + 512)
+                for g in range(4):
+                    nc.tensor.matmul_mx(
+                        out=acc[:],
+                        lhsT=cc[:, 128 * g : 128 * g + 128].bitcast(FP8X4),
+                        lhsT_scale=cs[:, 128 * g : 128 * g + 128],
+                        rhs=oW_c[:, g, ncols].bitcast(FP8X4),
+                        rhs_scale=oW_s[:, g, ncols],
+                        start=(g == 0),
+                        stop=(g == 3),
+                    )
+                nc.vector.scalar_tensor_tensor(
+                    out=h[:, ncols],
+                    in0=acc[:],
+                    scalar=1.0,
+                    in1=ob_b[:, ncols],
+                    op0=ALU.mult,
+                    op1=ALU.add,
+                    accum_out=sums[:, nh : nh + 1],
+                )
+            negmean = sm.tile([P, 1], F32, name="negmean", tag="negmean")
+            nc.vector.tensor_scalar(
+                out=negmean[:],
+                in0=sums[:, 0:1],
+                scalar1=sums[:, 1:2],
+                scalar2=-1.0 / D,
+                op0=ALU.add,
+                op1=ALU.mult,
+            )
+            hs[tau] = (h, negmean)
+
+        def back(tau):
+            b, sg = divmod(tau, 4)
+            h, negmean = hs[tau]
+            junk = up.tile([P, D], BF16, name="junk", tag="junk", bufs=1)
+            ssq = sm.tile([P, 1], F32, name="ssq", tag="ssq")
+            nc.scalar.activation(
+                out=junk[:], in_=h[:], func=ACT.Square, bias=negmean[:, 0:1], scale=1.0,
+                accum_out=ssq[:, 0:1],
+            )
+            std = sm.tile([P, 1], F32, name="std", tag="std")
+            nc.scalar.activation(
+                out=std[:], in_=ssq[:], func=ACT.Sqrt, bias=eps_t[:, 0:1], scale=1.0 / D
+            )
+            rstd = sm.tile([P, 1], F32, name="rstd", tag="rstd")
+            nc.vector.reciprocal(out=rstd[:], in_=std[:])
+            u = up.tile([P, D], F32, name="u", tag="u")
+            nc.vector.scalar_tensor_tensor(
+                out=u[:], in0=h[:], scalar=negmean[:, 0:1], in1=og_b[:], op0=ALU.add, op1=ALU.mult
+            )
+            nc.vector.scalar_tensor_tensor(
+                out=u[:], in0=u[:], scalar=rstd[:, 0:1], in1=be_b[:], op0=ALU.mult, op1=ALU.add
+            )
+            nc.scalar.activation(out=u[:], in_=u[:], func=ACT.Relu)
+            nc.sync.dma_start(out=out[b, 128 * sg : 128 * sg + 128, :], in_=u[:])
+
+        prep(0)
+        for tau in range(4):
+            stage1(tau)
+            prep_oW(tau)
+        for tau in range(4):
+            stage2(tau)
+        prep(1)
+        for tau in range(4, 8):
+            stage1(tau)
+            stage2(tau)
+        for tau in range(8):
+            back(tau)

@@ -3,10 +3,76 @@ from contextlib import ExitStack
 import concourse.mybir as mybir
 from concourse.masks import make_identity
 
+PINNED = True
+H_BUFS = 6
+U_BUFS = 4
+STEPS = (
+    ("ms",), ("ld", "A", 0), ("ld", "vp", 0), ("ld", "lp", 0),
+    ("ld", "oW", 0), ("ld", "oW", 1), ("ld", "oW", 2), ("ld", "oW", 3),
+    ("ld", "A", 1), ("ldc",), ("ta", 0, 0), ("reg", "A", 0, 0, "v"),
+    ("ld", "vp", 1), ("ta", 0, 1), ("tacp", 0, 0, "s"), ("obmm", 0),
+    ("tacp", 0, 1, "s"), ("obmm", 1), ("q", "A", 0, 0), ("cmm", "og"),
+    ("obcp", 1, "s"), ("q", "AT", 0, 0), ("ld", "lp", 1), ("cmm", "be"),
+    ("reg", "vp", 0, 1, "s"), ("obcp", 0, "v"), ("reg", "vp", 0, 0, "v"), ("q", "vp", 0, 0),
+    ("reg", "lp", 0, 1, "s"), ("q", "vp", 0, 1), ("s1", 0, 0), ("reg", "lp", 0, 0, "v"),
+    ("s1", 0, 1), ("q", "lp", 0, 0), ("p", 0, 0, "s"), ("q", "lp", 0, 1),
+    ("p", 0, 1, "s"), ("s1", 0, 2), ("reg", "oW", 0, 0, "v"), ("reg", "oW", 0, 1, "s"),
+    ("s1", 1, 0), ("s1", 0, 3), ("q", "oW", 0, 0), ("reg", "oW", 1, 0, "v"),
+    ("p", 0, 2, "s"), ("p", 0, 3, "s"), ("s1", 1, 1), ("q", "oW", 0, 1),
+    ("p", 1, 0, "s"), ("s1", 1, 2), ("qcb", 0), ("p", 1, 1, "s"),
+    ("s1", 1, 3), ("q", "oW", 1, 0), ("p", 1, 2, "s"), ("s1", 2, 0),
+    ("reg", "oW", 2, 0, "v"), ("p", 1, 3, "s"), ("s1", 2, 1), ("reg", "oW", 1, 1, "s"),
+    ("s1", 2, 2), ("qcb", 1), ("q", "oW", 2, 0), ("reg", "oW", 3, 0, "v"),
+    ("p", 2, 0, "s"), ("q", "oW", 1, 1), ("p", 2, 1, "s"), ("s1", 2, 3),
+    ("q", "oW", 3, 0), ("p", 2, 2, "s"), ("s1", 3, 0), ("reg", "A", 1, 0, "v"),
+    ("p", 2, 3, "s"), ("s1", 3, 1), ("s2", 0, 0), ("reg", "oW", 2, 1, "s"),
+    ("qcb", 2), ("s1", 3, 2), ("q", "A", 1, 0), ("s2", 1, 0),
+    ("a", 0, 0), ("p", 3, 0, "s"), ("q", "oW", 2, 1), ("p", 3, 1, "s"),
+    ("s1", 3, 3), ("a", 1, 0), ("p", 3, 2, "s"), ("ta", 1, 0),
+    ("reg", "vp", 1, 0, "v"), ("p", 3, 3, "s"), ("ta", 1, 1), ("reg", "oW", 3, 1, "s"),
+    ("qcb", 3), ("q", "vp", 1, 0), ("reg", "lp", 1, 0, "v"), ("tacp", 1, 0, "s"),
+    ("q", "oW", 3, 1), ("tacp", 1, 1, "s"), ("q", "lp", 1, 0), ("reg", "vp", 1, 1, "s"),
+    ("s2", 0, 1), ("q", "AT", 1, 0), ("s2", 1, 1), ("a", 0, 1),
+    ("reg", "lp", 1, 1, "s"), ("q", "vp", 1, 1), ("s2", 2, 0), ("nm", 0),
+    ("a", 1, 1), ("s2", 2, 1), ("c", 0, -1), ("b", 0),
+    ("s2", 3, 0), ("nm", 1), ("a", 2, 0), ("b", 1),
+    ("a", 2, 1), ("s2", 3, 1), ("a", 3, 0), ("sq", 0),
+    ("sq", 1), ("nm", 2), ("s1", 4, 0), ("q", "lp", 1, 1),
+    ("b", 2), ("s1", 4, 1), ("a", 3, 1), ("s1", 4, 2),
+    ("rc", 0), ("p", 4, 0, "s"), ("rc", 1), ("c", 1, -1),
+    ("p", 4, 1, "s"), ("s1", 4, 3), ("p", 4, 2, "s"), ("s1", 5, 0),
+    ("nm", 3), ("d", 0, -1), ("p", 4, 3, "s"), ("s1", 5, 1),
+    ("p", 5, 0, "s"), ("s1", 5, 2), ("qcb", 4), ("p", 5, 1, "s"),
+    ("s1", 5, 3), ("d", 1, -1), ("p", 5, 2, "s"), ("s1", 6, 0),
+    ("s2", 4, 0), ("p", 5, 3, "s"), ("c", 2, -1), ("p", 6, 0, "s"),
+    ("s2", 4, 1), ("e", 0, -1, "s"), ("a", 4, 0), ("s1", 6, 1),
+    ("qcb", 5), ("e", 1, -1, "s"), ("st", 0, -1), ("s1", 6, 2),
+    ("s1", 6, 3), ("a", 4, 1), ("s2", 5, 0), ("p", 6, 1, "s"),
+    ("c", 3, -1), ("st", 1, -1), ("p", 6, 2, "s"), ("s2", 5, 1),
+    ("p", 6, 3, "s"), ("nm", 4), ("a", 5, 0), ("sq", 2),
+    ("b", 3), ("s1", 7, 0), ("qcb", 6), ("s1", 7, 1),
+    ("s1", 7, 2), ("a", 5, 1), ("s2", 6, 0), ("p", 7, 0, "s"),
+    ("rc", 2), ("c", 4, -1), ("p", 7, 1, "s"), ("s2", 6, 1),
+    ("p", 7, 2, "s"), ("nm", 5), ("a", 6, 0), ("sq", 3),
+    ("b", 4), ("s1", 7, 3), ("d", 2, -1), ("p", 7, 3, "s"),
+    ("a", 6, 1), ("e", 2, -1, "s"), ("qcb", 7), ("nm", 6),
+    ("rc", 3), ("c", 5, -1), ("sq", 4), ("st", 2, -1),
+    ("s2", 7, 0), ("b", 5), ("d", 3, -1), ("s2", 7, 1),
+    ("b", 6), ("a", 7, 0), ("e", 3, -1, "s"), ("a", 7, 1),
+    ("rc", 4), ("c", 6, -1), ("sq", 5), ("st", 3, -1),
+    ("sq", 6), ("nm", 7), ("d", 4, -1), ("b", 7),
+    ("rc", 5), ("rc", 6), ("e", 4, -1, "s"), ("d", 5, -1),
+    ("sq", 7), ("st", 4, -1), ("d", 6, -1), ("e", 5, -1, "s"),
+    ("rc", 7), ("e", 6, -1, "s"), ("c", 7, 0), ("st", 5, -1),
+    ("d", 7, 0), ("st", 6, -1), ("c", 7, 1), ("e", 7, 0, "s"),
+    ("d", 7, 1), ("st", 7, 0), ("e", 7, 1, "s"), ("st", 7, 1),
+)
+
 F32 = mybir.dt.float32
 BF16 = mybir.dt.bfloat16
 U32 = mybir.dt.uint32
 U8 = mybir.dt.uint8
+I32 = mybir.dt.int32
 FP8X4 = mybir.dt.float8_e4m3fn_x4
 ALU = mybir.AluOpType
 ACT = mybir.ActivationFunctionType
@@ -16,21 +82,22 @@ B, S, D = 2, 512, 1024
 EPS = 1e-5
 FLOPS = 2 * (2 * B * S * S * D) + 2 * (B * S) * (2 * D) * D
 
-SPLIT2 = ("v", "s")
-
 
 def tile_clawmatrix_pb_kernel(tc, A, vp, lp, oW, ob, og, obeta, out):
     nc = tc.nc
     with ExitStack() as ctx:
         raw = ctx.enter_context(tc.tile_pool(name="raw", bufs=1))
-        grp = ctx.enter_context(tc.tile_pool(name="grp", bufs=6))
+        grp = ctx.enter_context(tc.tile_pool(name="grp", bufs=3))
         keep = ctx.enter_context(tc.tile_pool(name="keep", bufs=1))
         cbp = ctx.enter_context(tc.tile_pool(name="cbp", bufs=4))
-        hp = ctx.enter_context(tc.tile_pool(name="hp", bufs=8))
-        up = ctx.enter_context(tc.tile_pool(name="up", bufs=3))
+        hp = ctx.enter_context(tc.tile_pool(name="hp", bufs=H_BUFS))
+        up = ctx.enter_context(tc.tile_pool(name="up", bufs=U_BUFS))
         sm = ctx.enter_context(tc.tile_pool(name="sm", bufs=8))
-        ps1 = ctx.enter_context(tc.psum_pool(name="ps1", bufs=4))
-        ps2 = ctx.enter_context(tc.psum_pool(name="ps2", bufs=4))
+        ps1 = ctx.enter_context(tc.psum_pool(name="ps1", bufs=3))
+        ps2 = ctx.enter_context(tc.psum_pool(name="ps2", bufs=3))
+        psc = ctx.enter_context(tc.psum_pool(name="psc", bufs=1))
+        if PINNED:
+            ctx.enter_context(tc.manual_schedule())
 
         eps_t = keep.tile([P, 1], F32, name="eps_t")
         nc.vector.memset(eps_t[:], EPS)
@@ -39,215 +106,229 @@ def tile_clawmatrix_pb_kernel(tc, A, vp, lp, oW, ob, og, obeta, out):
         ident = keep.tile([P, P], F32, name="ident")
         make_identity(nc, ident[:])
 
-        A_sb, vp_sb, lp_sb = [], [], []
-
-        def load_batch(b):
-            a = raw.tile([P, 4, S], BF16, name="A_sb%d" % b)
-            nc.sync.dma_start(out=a[:], in_=A[b].rearrange("(t p) j -> p t j", p=P))
-            v = raw.tile([P, 4, D], BF16, name="vp_sb%d" % b)
-            for u in range(2):
-                nc.sync.dma_start(
-                    out=v[:, 2 * u : 2 * u + 2, :],
-                    in_=vp[b, 256 * u : 256 * u + 256, :].rearrange("(q e) d -> q e d", e=2),
-                )
-            l = raw.tile([P, 4, D], BF16, name="lp_sb%d" % b)
-            nc.sync.dma_start(out=l[:], in_=lp[b].rearrange("(t p) d -> p t d", p=P))
-            A_sb.append(a)
-            vp_sb.append(v)
-            lp_sb.append(l)
-
-        load_batch(0)
+        width = {"A": S, "AT": S, "vp": D, "lp": D, "oW": D}
+        codes = {}
+        scales = {}
+        for fam, count in (("A", 2), ("AT", 2), ("vp", 2), ("lp", 2), ("oW", 4)):
+            for i in range(count):
+                codes[(fam, i)] = keep.tile([P, width[fam]], U32, name="%s_c%d" % (fam, i), align_bytes=64)
+                scales[(fam, i)] = keep.tile([P, width[fam]], U8, name="%s_s%d" % (fam, i), align_bytes=64)
+        rawt = {}
+        rows = keep.tile([P, 3, D], BF16, name="rows")
+        ones = keep.tile([P, P], BF16, name="ones")
+        const = {"ob": keep.tile([P, D], F32, name="c_ob")}
+        stage = {}
+        bank = {}
+        cb = {}
+        acc = {}
+        ht = {}
+        ut = {}
+        small = {}
         oW_v = oW.rearrange("(g t p) n -> g p t n", t=4, p=P)
-        oW_sb = []
-        for g in range(4):
-            w = raw.tile([P, 4, D], BF16, name="oW_sb%d" % g)
-            nc.sync.dma_start(out=w[:], in_=oW_v[g])
-            oW_sb.append(w)
-        ob_b = keep.tile([P, D], BF16, name="ob_b")
-        nc.sync.dma_start(out=ob_b[:], in_=ob.partition_broadcast(P))
-        load_batch(1)
-        og_b = keep.tile([P, D], BF16, name="og_b")
-        nc.sync.dma_start(out=og_b[:], in_=og.partition_broadcast(P))
-        be_b = keep.tile([P, D], BF16, name="be_b")
-        nc.sync.dma_start(out=be_b[:], in_=obeta.partition_broadcast(P))
 
-        def regroup(eng, src):
-            g = grp.tile([P, 512, 4], BF16, name="g", tag="grp", align_bytes=64)
-            d4 = g[:].rearrange("p (c i) t -> p c t i", i=4)
-            s4 = src.rearrange("p t (c i) -> p c t i", i=4)
+        def copy(eng, dst, src):
             if eng == "v":
-                nc.vector.tensor_copy(out=d4, in_=s4)
+                nc.vector.tensor_copy(out=dst, in_=src)
             else:
-                nc.scalar.copy(out=d4, in_=s4)
-            return g
+                nc.scalar.copy(out=dst, in_=src)
 
-        def quantise(g, codes, scales):
-            nc.vector.quantize_mx(
-                out=codes.bitcast(FP8X4),
-                scales=scales,
-                in_=g,
-            )
+        def cols(half):
+            return slice(0, D) if half < 0 else slice(512 * half, 512 * half + 512)
 
-        def kfirst(src, width, codes, scales, engs):
-            gs = []
-            for c in range(width // 512):
-                gs.append(regroup(engs[c % len(engs)], src[:, :, 512 * c : 512 * c + 512]))
-            for c in range(width // 512):
-                quantise(
-                    gs[c][:].rearrange("p w t -> p (w t)"),
-                    codes[:, 512 * c : 512 * c + 512],
-                    scales[:, 512 * c : 512 * c + 512],
-                )
-
-        AT_c, AT_s, A_c, A_s, vp_c, vp_s, lp_c, lp_s = [], [], [], [], [], [], [], []
-
-        def prep(b):
-            atc = keep.tile([P, S], U32, name="AT_c%d" % b, align_bytes=64)
-            ats = keep.tile([P, S], U8, name="AT_s%d" % b, align_bytes=64)
-            ac = keep.tile([P, S], U32, name="A_c%d" % b, align_bytes=64)
-            as_ = keep.tile([P, S], U8, name="A_s%d" % b, align_bytes=64)
-            vc = keep.tile([P, D], U32, name="vp_c%d" % b, align_bytes=64)
-            vs = keep.tile([P, D], U8, name="vp_s%d" % b, align_bytes=64)
-            lc = keep.tile([P, D], U32, name="lp_c%d" % b, align_bytes=64)
-            ls = keep.tile([P, D], U8, name="lp_s%d" % b, align_bytes=64)
-            gt = grp.tile([P, 512, 4], BF16, name="gt", tag="grp", align_bytes=64)
-            g32 = gt[:].rearrange("p w t -> p (w t)").bitcast(F32).rearrange("p (i u) -> p i u", u=2)
-            for half in range(2):
+        def step(s):
+            kind = s[0]
+            if kind == "ld":
+                fam, i = s[1], s[2]
+                t = raw.tile([P, 4, width[fam]], BF16, name="raw_%s%d" % (fam, i))
+                rawt[(fam, i)] = t
+                if fam == "A":
+                    nc.sync.dma_start(out=t[:], in_=A[i].rearrange("(t p) j -> p t j", p=P))
+                elif fam == "lp":
+                    nc.sync.dma_start(out=t[:], in_=lp[i].rearrange("(t p) d -> p t d", p=P))
+                elif fam == "oW":
+                    nc.sync.dma_start(out=t[:], in_=oW_v[i])
+                else:
+                    for u in range(2):
+                        nc.sync.dma_start(
+                            out=t[:, 2 * u : 2 * u + 2, :],
+                            in_=vp[i, 256 * u : 256 * u + 256, :].rearrange("(q e) d -> q e d", e=2),
+                        )
+            elif kind == "ms":
+                nc.vector.memset(rows[:].rearrange("p a d -> p (a d)").bitcast(I32), 0)
+                nc.vector.memset(ones[:], 1.0)
+            elif kind == "ldc":
+                for i, vec in enumerate((ob, og, obeta)):
+                    nc.scalar.dma_start(out=rows[0:1, i, :], in_=vec.unsqueeze(0))
+            elif kind == "cmm":
+                t = psc.tile([P, D], BF16, name="c_" + s[1])
+                const[s[1]] = t
+                for nh in range(2):
+                    nc.tensor.matmul(
+                        out=t[:, cols(nh)], lhsT=ones[:], rhs=rows[:, {"og": 1, "be": 2}[s[1]], cols(nh)], start=True, stop=True
+                    )
+            elif kind == "obmm":
+                a = ps2.tile([P, 512], F32, name="obp", tag="s2")
+                acc[("ob", s[1])] = a
+                nc.tensor.matmul(out=a[:], lhsT=ones[:], rhs=rows[:, 0, cols(s[1])], start=True, stop=True)
+            elif kind == "obcp":
+                copy(s[2], const["ob"][:, cols(s[1])], acc[("ob", s[1])][:])
+            elif kind == "ta":
+                b, half = s[1], s[2]
                 xt = ps1.tile([P, 2, 256], F32, name="xt", tag="s1")
+                bank[("ta", b, half)] = xt
                 for u in range(2):
                     for hh in range(2):
-                        it = 2 * half + hh
                         nc.tensor.transpose(
                             xt[:, u, 128 * hh : 128 * hh + 128],
-                            A_sb[b][:, it, :].bitcast(F32)[:, 128 * u : 128 * u + 128],
+                            rawt[("A", b)][:, 2 * half + hh, :].bitcast(F32)[:, 128 * u : 128 * u + 128],
                             ident[:],
                         )
-                nc.scalar.copy(
-                    out=g32[:, 256 * half : 256 * half + 256, :],
-                    in_=xt[:].rearrange("p u i -> p i u"),
+            elif kind == "tacp":
+                b, half = s[1], s[2]
+                if ("AT", b, 0) not in stage:
+                    stage[("AT", b, 0)] = grp.tile([P, 2048], BF16, name="gt", tag="gs", align_bytes=64)
+                g32 = stage[("AT", b, 0)][:].bitcast(F32).rearrange("p (i u) -> p i u", u=2)
+                copy(s[3], g32[:, 256 * half : 256 * half + 256, :], bank[("ta", b, half)][:].rearrange("p u i -> p i u"))
+            elif kind == "reg":
+                fam, i, unit, eng = s[1], s[2], s[3], s[4]
+                g = grp.tile([P, 2048], BF16, name="g" + eng, tag="g" + eng, align_bytes=64)
+                stage[(fam, i, unit)] = g
+                copy(
+                    eng,
+                    g[:].rearrange("p (c i t) -> p c t i", i=4, t=4),
+                    rawt[(fam, i)][:, :, 512 * unit : 512 * unit + 512].rearrange("p t (c i) -> p c t i", i=4),
                 )
-            ga = regroup("v", A_sb[b][:, :, :])
-            quantise(ga[:].rearrange("p w t -> p (w t)"), ac[:], as_[:])
-            quantise(gt[:].rearrange("p w t -> p (w t)"), atc[:], ats[:])
-            kfirst(vp_sb[b], D, vc, vs, SPLIT2)
-            kfirst(lp_sb[b], D, lc, ls, SPLIT2)
-            AT_c.append(atc)
-            AT_s.append(ats)
-            A_c.append(ac)
-            A_s.append(as_)
-            vp_c.append(vc)
-            vp_s.append(vs)
-            lp_c.append(lc)
-            lp_s.append(ls)
-
-        oW_c = keep.tile([P, 4, D], U32, name="oW_c", align_bytes=64)
-        oW_s = keep.tile([P, 4, D], U8, name="oW_s", align_bytes=64)
-
-        def prep_oW(g):
-            kfirst(oW_sb[g], D, oW_c[:, g, :], oW_s[:, g, :], SPLIT2)
-
-        cb = {}
-
-        def stage1(tau):
-            b, sg = divmod(tau, 4)
-            cols = slice(128 * sg, 128 * sg + 128)
-            cbg = grp.tile([P, 4, 128, 4], BF16, name="cbg", tag="grp", align_bytes=64)
-            for g in range(4):
-                if g < 2:
-                    wc, ws, rc, rs = vp_c[b], vp_s[b], AT_c[b], AT_s[b]
-                else:
-                    wc, ws, rc, rs = lp_c[b], lp_s[b], A_c[b], A_s[b]
-                bank = ps1.tile([P, 4, 128], F32, name="bank", tag="s1")
+            elif kind == "q":
+                fam, i, unit = s[1], s[2], s[3]
+                w = slice(512 * unit, 512 * unit + 512)
+                nc.vector.quantize_mx(
+                    out=codes[(fam, i)][:, w].bitcast(FP8X4), scales=scales[(fam, i)][:, w], in_=stage[(fam, i, unit)][:]
+                )
+            elif kind == "s1":
+                tau, g = s[1], s[2]
+                b, sg = divmod(tau, 4)
+                wf, rf = ("vp", "AT") if g < 2 else ("lp", "A")
+                bk = ps1.tile([P, 4, 128], F32, name="bank", tag="s1")
+                bank[("s1", tau, g)] = bk
                 for t in range(4):
                     c0 = 128 * (4 * (g % 2) + t)
                     nc.tensor.matmul_mx(
-                        out=bank[:, t, :],
-                        lhsT=wc[:, c0 : c0 + 128].bitcast(FP8X4),
-                        lhsT_scale=ws[:, c0 : c0 + 128],
-                        rhs=rc[:, cols].bitcast(FP8X4),
-                        rhs_scale=rs[:, cols],
+                        out=bk[:, t, :],
+                        lhsT=codes[(wf, b)][:, c0 : c0 + 128].bitcast(FP8X4),
+                        lhsT_scale=scales[(wf, b)][:, c0 : c0 + 128],
+                        rhs=codes[(rf, b)][:, 128 * sg : 128 * sg + 128].bitcast(FP8X4),
+                        rhs_scale=scales[(rf, b)][:, 128 * sg : 128 * sg + 128],
                         start=True,
                         stop=True,
                     )
-                nc.scalar.copy(out=cbg[:, g, :, :], in_=bank[:].rearrange("p t s -> p s t"))
-            cc = cbp.tile([P, 512], U32, name="cb_c", tag="cb_c", align_bytes=64)
-            cs = cbp.tile([P, 512], U8, name="cb_s", tag="cb_s", align_bytes=64)
-            quantise(cbg[:].rearrange("p g s t -> p (g s t)"), cc[:], cs[:])
-            cb[tau] = (cc, cs)
-
-        hs = {}
-
-        def stage2(tau):
-            cc, cs = cb[tau]
-            h = hp.tile([P, D], F32, name="h", tag="h")
-            sums = sm.tile([P, 2], F32, name="sums", tag="sums")
-            for nh in range(2):
-                acc = ps2.tile([P, 512], F32, name="acc", tag="s2")
-                ncols = slice(512 * nh, 512 * nh + 512)
+            elif kind == "p":
+                tau, g = s[1], s[2]
+                if ("cb", tau) not in stage:
+                    stage[("cb", tau)] = grp.tile([P, 4, 128, 4], BF16, name="gc", tag="gc", align_bytes=64)
+                copy(s[3], stage[("cb", tau)][:, g, :, :], bank[("s1", tau, g)][:].rearrange("p t s -> p s t"))
+            elif kind == "qcb":
+                tau = s[1]
+                cc = cbp.tile([P, 512], U32, name="cb_c", tag="cb_c", align_bytes=64)
+                cs = cbp.tile([P, 512], U8, name="cb_s", tag="cb_s", align_bytes=64)
+                cb[tau] = (cc, cs)
+                nc.vector.quantize_mx(
+                    out=cc[:].bitcast(FP8X4), scales=cs[:], in_=stage[("cb", tau)][:].rearrange("p g s t -> p (g s t)")
+                )
+            elif kind == "s2":
+                tau, nh = s[1], s[2]
+                cc, cs = cb[tau]
+                a = ps2.tile([P, 512], F32, name="acc", tag="s2")
+                acc[(tau, nh)] = a
                 for g in range(4):
                     nc.tensor.matmul_mx(
-                        out=acc[:],
+                        out=a[:],
                         lhsT=cc[:, 128 * g : 128 * g + 128].bitcast(FP8X4),
                         lhsT_scale=cs[:, 128 * g : 128 * g + 128],
-                        rhs=oW_c[:, g, ncols].bitcast(FP8X4),
-                        rhs_scale=oW_s[:, g, ncols],
+                        rhs=codes[("oW", g)][:, cols(nh)].bitcast(FP8X4),
+                        rhs_scale=scales[("oW", g)][:, cols(nh)],
                         start=(g == 0),
                         stop=(g == 3),
                     )
+            elif kind == "a":
+                tau, nh = s[1], s[2]
+                if tau not in ht:
+                    ht[tau] = hp.tile([P, D], F32, name="h", tag="h")
+                    small[("sums", tau)] = sm.tile([P, 2], F32, name="sums", tag="sums")
                 nc.vector.scalar_tensor_tensor(
-                    out=h[:, ncols],
-                    in0=acc[:],
+                    out=ht[tau][:, cols(nh)],
+                    in0=acc[(tau, nh)][:],
                     scalar=1.0,
-                    in1=ob_b[:, ncols],
+                    in1=const["ob"][:, cols(nh)],
                     op0=ALU.mult,
                     op1=ALU.add,
-                    accum_out=sums[:, nh : nh + 1],
+                    accum_out=small[("sums", tau)][:, nh : nh + 1],
                 )
-            negmean = sm.tile([P, 1], F32, name="negmean", tag="negmean")
-            nc.vector.tensor_scalar(
-                out=negmean[:],
-                in0=sums[:, 0:1],
-                scalar1=sums[:, 1:2],
-                scalar2=-1.0 / D,
-                op0=ALU.add,
-                op1=ALU.mult,
-            )
-            hs[tau] = (h, negmean)
+            elif kind == "nm":
+                tau = s[1]
+                small[("nm", tau)] = sm.tile([P, 1], F32, name="negmean", tag="negmean")
+                nc.vector.tensor_scalar(
+                    out=small[("nm", tau)][:],
+                    in0=small[("sums", tau)][:, 0:1],
+                    scalar1=small[("sums", tau)][:, 1:2],
+                    scalar2=-1.0 / D,
+                    op0=ALU.add,
+                    op1=ALU.mult,
+                )
+            elif kind == "b":
+                tau = s[1]
+                junk = up.tile([P, D], BF16, name="junk", tag="junk", bufs=1)
+                small[("ssq", tau)] = sm.tile([P, 1], F32, name="ssq", tag="ssq")
+                nc.scalar.activation(
+                    out=junk[:],
+                    in_=ht[tau][:],
+                    func=ACT.Square,
+                    bias=small[("nm", tau)][:, 0:1],
+                    scale=1.0,
+                    accum_out=small[("ssq", tau)][:, 0:1],
+                )
+            elif kind == "sq":
+                tau = s[1]
+                small[("std", tau)] = sm.tile([P, 1], F32, name="std", tag="std")
+                nc.scalar.activation(
+                    out=small[("std", tau)][:], in_=small[("ssq", tau)][:], func=ACT.Sqrt, bias=eps_t[:, 0:1], scale=1.0 / D
+                )
+            elif kind == "rc":
+                tau = s[1]
+                small[("rstd", tau)] = sm.tile([P, 1], F32, name="rstd", tag="rstd")
+                nc.vector.reciprocal(out=small[("rstd", tau)][:], in_=small[("std", tau)][:])
+            elif kind == "c":
+                tau, w = s[1], cols(s[2])
+                if tau not in ut:
+                    ut[tau] = up.tile([P, D], F32, name="u", tag="u")
+                nc.vector.scalar_tensor_tensor(
+                    out=ut[tau][:, w],
+                    in0=ht[tau][:, w],
+                    scalar=small[("nm", tau)][:, 0:1],
+                    in1=const["og"][:, w],
+                    op0=ALU.add,
+                    op1=ALU.mult,
+                )
+            elif kind == "d":
+                tau, w = s[1], cols(s[2])
+                nc.vector.scalar_tensor_tensor(
+                    out=ut[tau][:, w],
+                    in0=ut[tau][:, w],
+                    scalar=small[("rstd", tau)][:, 0:1],
+                    in1=const["be"][:, w],
+                    op0=ALU.mult,
+                    op1=ALU.add,
+                )
+            elif kind == "e":
+                tau, w = s[1], cols(s[2])
+                if s[3] == "v":
+                    nc.vector.tensor_scalar_max(out=ut[tau][:, w], in0=ut[tau][:, w], scalar1=0.0)
+                else:
+                    nc.scalar.activation(out=ut[tau][:, w], in_=ut[tau][:, w], func=ACT.Relu)
+            else:
+                assert kind == "st"
+                tau, w = s[1], cols(s[2])
+                b, sg = divmod(tau, 4)
+                nc.sync.dma_start(out=out[b, 128 * sg : 128 * sg + 128, w], in_=ut[tau][:, w])
 
-        def back(tau):
-            b, sg = divmod(tau, 4)
-            h, negmean = hs[tau]
-            junk = up.tile([P, D], BF16, name="junk", tag="junk", bufs=1)
-            ssq = sm.tile([P, 1], F32, name="ssq", tag="ssq")
-            nc.scalar.activation(
-                out=junk[:], in_=h[:], func=ACT.Square, bias=negmean[:, 0:1], scale=1.0,
-                accum_out=ssq[:, 0:1],
-            )
-            std = sm.tile([P, 1], F32, name="std", tag="std")
-            nc.scalar.activation(
-                out=std[:], in_=ssq[:], func=ACT.Sqrt, bias=eps_t[:, 0:1], scale=1.0 / D
-            )
-            rstd = sm.tile([P, 1], F32, name="rstd", tag="rstd")
-            nc.vector.reciprocal(out=rstd[:], in_=std[:])
-            u = up.tile([P, D], F32, name="u", tag="u")
-            nc.vector.scalar_tensor_tensor(
-                out=u[:], in0=h[:], scalar=negmean[:, 0:1], in1=og_b[:], op0=ALU.add, op1=ALU.mult
-            )
-            nc.vector.scalar_tensor_tensor(
-                out=u[:], in0=u[:], scalar=rstd[:, 0:1], in1=be_b[:], op0=ALU.mult, op1=ALU.add
-            )
-            nc.scalar.activation(out=u[:], in_=u[:], func=ACT.Relu)
-            nc.sync.dma_start(out=out[b, 128 * sg : 128 * sg + 128, :], in_=u[:])
-
-        prep(0)
-        for tau in range(4):
-            stage1(tau)
-            prep_oW(tau)
-        for tau in range(4):
-            stage2(tau)
-        prep(1)
-        for tau in range(4, 8):
-            stage1(tau)
-            stage2(tau)
-        for tau in range(8):
-            back(tau)
+        for s in STEPS:
+            step(s)

@@ -3,71 +3,6 @@ from contextlib import ExitStack
 import concourse.mybir as mybir
 from concourse.masks import make_identity
 
-PINNED = True
-H_BUFS = 6
-U_BUFS = 4
-STEPS = (
-    ("ms",), ("ld", "A", 0), ("ld", "vp", 0), ("ld", "lp", 0),
-    ("ld", "oW", 0), ("ld", "oW", 1), ("ld", "oW", 2), ("ld", "oW", 3),
-    ("ld", "A", 1), ("ldc",), ("ta", 0, 0), ("reg", "A", 0, 0, "v"),
-    ("ld", "vp", 1), ("ta", 0, 1), ("tacp", 0, 0, "s"), ("obmm", 0),
-    ("tacp", 0, 1, "s"), ("obmm", 1), ("q", "A", 0, 0), ("cmm", "og"),
-    ("obcp", 1, "s"), ("q", "AT", 0, 0), ("ld", "lp", 1), ("cmm", "be"),
-    ("reg", "vp", 0, 1, "s"), ("obcp", 0, "v"), ("reg", "vp", 0, 0, "v"), ("q", "vp", 0, 0),
-    ("reg", "lp", 0, 1, "s"), ("q", "vp", 0, 1), ("s1", 0, 0), ("reg", "lp", 0, 0, "v"),
-    ("s1", 0, 1), ("q", "lp", 0, 0), ("p", 0, 0, "s"), ("q", "lp", 0, 1),
-    ("p", 0, 1, "s"), ("s1", 0, 2), ("reg", "oW", 0, 0, "v"), ("reg", "oW", 0, 1, "s"),
-    ("s1", 1, 0), ("s1", 0, 3), ("q", "oW", 0, 0), ("reg", "oW", 1, 0, "v"),
-    ("p", 0, 2, "s"), ("p", 0, 3, "s"), ("s1", 1, 1), ("q", "oW", 0, 1),
-    ("p", 1, 0, "s"), ("s1", 1, 2), ("qcb", 0), ("p", 1, 1, "s"),
-    ("s1", 1, 3), ("q", "oW", 1, 0), ("p", 1, 2, "s"), ("s1", 2, 0),
-    ("reg", "oW", 2, 0, "v"), ("p", 1, 3, "s"), ("s1", 2, 1), ("reg", "oW", 1, 1, "s"),
-    ("s1", 2, 2), ("qcb", 1), ("q", "oW", 2, 0), ("reg", "oW", 3, 0, "v"),
-    ("p", 2, 0, "s"), ("q", "oW", 1, 1), ("p", 2, 1, "s"), ("s1", 2, 3),
-    ("q", "oW", 3, 0), ("p", 2, 2, "s"), ("s1", 3, 0), ("reg", "A", 1, 0, "v"),
-    ("p", 2, 3, "s"), ("s1", 3, 1), ("s2", 0, 0), ("reg", "oW", 2, 1, "s"),
-    ("qcb", 2), ("s1", 3, 2), ("q", "A", 1, 0), ("s2", 1, 0),
-    ("a", 0, 0), ("p", 3, 0, "s"), ("q", "oW", 2, 1), ("p", 3, 1, "s"),
-    ("s1", 3, 3), ("a", 1, 0), ("p", 3, 2, "s"), ("ta", 1, 0),
-    ("reg", "vp", 1, 0, "v"), ("p", 3, 3, "s"), ("ta", 1, 1), ("reg", "oW", 3, 1, "s"),
-    ("qcb", 3), ("q", "vp", 1, 0), ("reg", "lp", 1, 0, "v"), ("tacp", 1, 0, "s"),
-    ("q", "oW", 3, 1), ("tacp", 1, 1, "s"), ("q", "lp", 1, 0), ("reg", "vp", 1, 1, "s"),
-    ("s2", 0, 1), ("q", "AT", 1, 0), ("s2", 1, 1), ("a", 0, 1),
-    ("reg", "lp", 1, 1, "s"), ("q", "vp", 1, 1), ("s2", 2, 0), ("nm", 0),
-    ("a", 1, 1), ("s2", 2, 1), ("c", 0, -1), ("b", 0),
-    ("s2", 3, 0), ("nm", 1), ("a", 2, 0), ("b", 1),
-    ("a", 2, 1), ("s2", 3, 1), ("a", 3, 0), ("sq", 0),
-    ("sq", 1), ("nm", 2), ("s1", 4, 0), ("q", "lp", 1, 1),
-    ("b", 2), ("s1", 4, 1), ("a", 3, 1), ("s1", 4, 2),
-    ("rc", 0), ("p", 4, 0, "s"), ("rc", 1), ("c", 1, -1),
-    ("p", 4, 1, "s"), ("s1", 4, 3), ("p", 4, 2, "s"), ("s1", 5, 0),
-    ("nm", 3), ("d", 0, -1), ("p", 4, 3, "s"), ("s1", 5, 1),
-    ("p", 5, 0, "s"), ("s1", 5, 2), ("qcb", 4), ("p", 5, 1, "s"),
-    ("s1", 5, 3), ("d", 1, -1), ("p", 5, 2, "s"), ("s1", 6, 0),
-    ("s2", 4, 0), ("p", 5, 3, "s"), ("c", 2, -1), ("p", 6, 0, "s"),
-    ("s2", 4, 1), ("e", 0, -1, "s"), ("a", 4, 0), ("s1", 6, 1),
-    ("qcb", 5), ("e", 1, -1, "s"), ("st", 0, -1), ("s1", 6, 2),
-    ("s1", 6, 3), ("a", 4, 1), ("s2", 5, 0), ("p", 6, 1, "s"),
-    ("c", 3, -1), ("st", 1, -1), ("p", 6, 2, "s"), ("s2", 5, 1),
-    ("p", 6, 3, "s"), ("nm", 4), ("a", 5, 0), ("sq", 2),
-    ("b", 3), ("s1", 7, 0), ("qcb", 6), ("s1", 7, 1),
-    ("s1", 7, 2), ("a", 5, 1), ("s2", 6, 0), ("p", 7, 0, "s"),
-    ("rc", 2), ("c", 4, -1), ("p", 7, 1, "s"), ("s2", 6, 1),
-    ("p", 7, 2, "s"), ("nm", 5), ("a", 6, 0), ("sq", 3),
-    ("b", 4), ("s1", 7, 3), ("d", 2, -1), ("p", 7, 3, "s"),
-    ("a", 6, 1), ("e", 2, -1, "s"), ("qcb", 7), ("nm", 6),
-    ("rc", 3), ("c", 5, -1), ("sq", 4), ("st", 2, -1),
-    ("s2", 7, 0), ("b", 5), ("d", 3, -1), ("s2", 7, 1),
-    ("b", 6), ("a", 7, 0), ("e", 3, -1, "s"), ("a", 7, 1),
-    ("rc", 4), ("c", 6, -1), ("sq", 5), ("st", 3, -1),
-    ("sq", 6), ("nm", 7), ("d", 4, -1), ("b", 7),
-    ("rc", 5), ("rc", 6), ("e", 4, -1, "s"), ("d", 5, -1),
-    ("sq", 7), ("st", 4, -1), ("d", 6, -1), ("e", 5, -1, "s"),
-    ("rc", 7), ("e", 6, -1, "s"), ("c", 7, 0), ("st", 5, -1),
-    ("d", 7, 0), ("st", 6, -1), ("c", 7, 1), ("e", 7, 0, "s"),
-    ("d", 7, 1), ("st", 7, 0), ("e", 7, 1, "s"), ("st", 7, 1),
-)
-
 F32 = mybir.dt.float32
 BF16 = mybir.dt.bfloat16
 U32 = mybir.dt.uint32
@@ -81,6 +16,14 @@ P = 128
 B, S, D = 2, 512, 1024
 EPS = 1e-5
 FLOPS = 2 * (2 * B * S * S * D) + 2 * (B * S) * (2 * D) * D
+TILES = 8
+CB = 4
+H = 4
+U = 4
+N1 = 4
+N2 = 4
+PE_SHIFT = ()
+RELU_V = (7,)
 
 
 def tile_clawmatrix_pb_kernel(tc, A, vp, lp, oW, ob, og, obeta, out):
@@ -89,20 +32,82 @@ def tile_clawmatrix_pb_kernel(tc, A, vp, lp, oW, ob, og, obeta, out):
         raw = ctx.enter_context(tc.tile_pool(name="raw", bufs=1))
         grp = ctx.enter_context(tc.tile_pool(name="grp", bufs=3))
         keep = ctx.enter_context(tc.tile_pool(name="keep", bufs=1))
-        cbp = ctx.enter_context(tc.tile_pool(name="cbp", bufs=4))
-        hp = ctx.enter_context(tc.tile_pool(name="hp", bufs=H_BUFS))
-        up = ctx.enter_context(tc.tile_pool(name="up", bufs=U_BUFS))
+        cbp = ctx.enter_context(tc.tile_pool(name="cbp", bufs=CB))
+        hp = ctx.enter_context(tc.tile_pool(name="hp", bufs=H))
+        up = ctx.enter_context(tc.tile_pool(name="up", bufs=U))
         sm = ctx.enter_context(tc.tile_pool(name="sm", bufs=8))
-        ps1 = ctx.enter_context(tc.psum_pool(name="ps1", bufs=3))
-        ps2 = ctx.enter_context(tc.psum_pool(name="ps2", bufs=3))
-        psc = ctx.enter_context(tc.psum_pool(name="psc", bufs=1))
-        if PINNED:
-            ctx.enter_context(tc.manual_schedule())
+        ps1 = ctx.enter_context(tc.psum_pool(name="ps1", bufs=N1))
+        ps2 = ctx.enter_context(tc.psum_pool(name="ps2", bufs=N2))
+        ctx.enter_context(tc.manual_schedule())
+
+        LOADS = [("load", "A", 0), ("load", "vp", 0), ("load", "lp", 0)] + [("load", "oW", g) for g in range(4)]
+        LOADS += [("load", "A", 1), ("load", "vp", 1), ("load", "lp", 1)]
+        OW_S = [("oW", 0, 1), ("oW", 1, 1)]
+        B1_S = [("vp", 1, 1), ("lp", 1, 1)]
+        OW_V = [("oW", g, u) for u in range(2) for g in range(4) if ("oW", g, u) not in OW_S]
+        ON_VECTOR = [("A", 0, 0), ("A", 1, 0), ("vp", 0, 0), ("lp", 0, 0), ("vp", 1, 0), ("lp", 1, 0)] + OW_V
+        FRONT0 = [(t, g) for t in range(4) for g in range(4)]
+        FRONT1 = [(t, g) for t in range(4, 8) for g in range(4)]
+
+        SCALAR = [("turned", 0, 0), ("turned", 0, 1), ("reg", "vp", 0, 1), ("obc", 0), ("obc", 1), ("reg", "lp", 0, 1)]
+        SCALAR += [("reg",) + u for u in OW_S[:2]] + [("pack",) + x for x in FRONT0[:4]]
+        SCALAR += [("pack",) + x for x in FRONT0[4:]] + [("rowc", 1), ("rowc", 2)]
+        items = [("turned", 1, 0), ("turned", 1, 1)] + [("piece",) + u + (k,) for u in B1_S for k in range(4)]
+        items += [("pack",) + x for x in FRONT1]
+        PER = (5, 6, 5, 4, 3, 3, 0, 0, 0, 0)
+        MINE = []
+        for r in range(10):
+            mine, items = items[: PER[r]], items[PER[r] :]
+            MINE.append(mine)
+            if 0 < r < 9:
+                SCALAR += [("nm", r - 1), ("b", r - 1), ("rs", r - 1)]
+            SCALAR += mine
+            if 1 < r < 9:
+                SCALAR += [("e", r - 2, -1)]
+        GPSIMD = []
+        STORES = [("st", r, -1) for r in range(7)] + [("st", 7, 0), ("st", 7, 1)]
+
+        VECTOR = [("reg", "A", 0, 0), ("q", "A", 0, 0), ("reg", "vp", 0, 0), ("q", "AT", 0, 0), ("q", "vp", 0, 0)]
+        VECTOR += [("reg", "lp", 0, 0), ("q", "vp", 0, 1), ("q", "lp", 0, 0)]
+        ow = [("reg",) + u for u in OW_V]
+        oq = [("q",) + u for u in OW_V]
+        sq = [("q",) + u for u in OW_S]
+        VECTOR += [ow[0], ("q", "lp", 0, 1), ow[1], oq[0], sq[0], ow[2], oq[1], sq[1], ow[3], oq[2], ow[4], oq[3], ("qcb", 0), ow[5], oq[4], oq[5]]
+        VECTOR += [("reg", "A", 1, 0), ("qcb", 1), ("q", "A", 1, 0), ("qcb", 2)]
+        FILL = {
+            0: [("reg", "vp", 1, 0), ("qcb", 3)],
+            1: [("q", "AT", 1, 0), ("reg", "lp", 1, 0), ("q", "vp", 1, 0), ("q", "vp", 1, 1), ("q", "lp", 1, 0), ("q", "lp", 1, 1)],
+            3: [("qcb", 4)],
+            4: [("qcb", 5)],
+            5: [("qcb", 6)],
+            6: [("qcb", 7)],
+        }
+        for r in range(10):
+            f = FILL.get(r, [])
+            VECTOR += [("a", r, 0)] if r < 8 else []
+            VECTOR += f[:1]
+            VECTOR += [("d", r - 2, -1)] if 1 < r < 9 else []
+            VECTOR += [("a", r, 1)] if r < 8 else []
+            VECTOR += f[1:2]
+            VECTOR += [("c", r - 1, -1)] if 0 < r < 9 else []
+            VECTOR += f[2:]
+        VECTOR += [("d", 7, 0), ("d", 7, 1), ("e", 7, 0), ("e", 7, 1)]
+
+        TENSOR = [("turn", 0, 0), ("turn", 0, 1), ("ob", 0), ("ob", 1), ("row", 1), ("row", 2)]
+        TENSOR += [("s1",) + x for x in FRONT0] + [("s2", 0, 0), ("s2", 0, 1), ("turn", 1, 0), ("turn", 1, 1)]
+        s1s = [("s1",) + x for x in FRONT1]
+        sent, packed = 0, 0
+        for r in range(8):
+            TENSOR += [("s2", r + 1, 0), ("s2", r + 1, 1)] if r < 7 else []
+            packed += len([x for x in MINE[r] if x[0] == "pack"])
+            upto = min(16, packed + N1) if packed else 0
+            TENSOR += s1s[sent:upto]
+            sent = upto
 
         eps_t = keep.tile([P, 1], F32, name="eps_t")
         nc.vector.memset(eps_t[:], EPS)
         warm = keep.tile([P, 1], F32, name="warm")
-        nc.scalar.activation(out=warm[:], in_=eps_t[:], func=ACT.Sqrt)
+        nc.scalar.activation(out=warm[:], in_=eps_t[:], func=ACT.Abs_reciprocal_sqrt)
         ident = keep.tile([P, P], F32, name="ident")
         make_identity(nc, ident[:])
 
@@ -116,7 +121,7 @@ def tile_clawmatrix_pb_kernel(tc, A, vp, lp, oW, ob, og, obeta, out):
         rawt = {}
         rows = keep.tile([P, 3, D], BF16, name="rows")
         ones = keep.tile([P, P], BF16, name="ones")
-        const = {"ob": keep.tile([P, D], F32, name="c_ob")}
+        ob_t = keep.tile([P, D], F32, name="ob_t")
         stage = {}
         bank = {}
         cb = {}
@@ -124,7 +129,11 @@ def tile_clawmatrix_pb_kernel(tc, A, vp, lp, oW, ob, og, obeta, out):
         ht = {}
         ut = {}
         small = {}
+        const = {}
         oW_v = oW.rearrange("(g t p) n -> g p t n", t=4, p=P)
+
+        def cols(half):
+            return slice(0, D) if half < 0 else slice(512 * half, 512 * half + 512)
 
         def copy(eng, dst, src):
             if eng == "v":
@@ -132,203 +141,320 @@ def tile_clawmatrix_pb_kernel(tc, A, vp, lp, oW, ob, og, obeta, out):
             else:
                 nc.scalar.copy(out=dst, in_=src)
 
-        def cols(half):
-            return slice(0, D) if half < 0 else slice(512 * half, 512 * half + 512)
-
-        def step(s):
-            kind = s[0]
-            if kind == "ld":
-                fam, i = s[1], s[2]
-                t = raw.tile([P, 4, width[fam]], BF16, name="raw_%s%d" % (fam, i))
-                rawt[(fam, i)] = t
-                if fam == "A":
-                    nc.sync.dma_start(out=t[:], in_=A[i].rearrange("(t p) j -> p t j", p=P))
-                elif fam == "lp":
-                    nc.sync.dma_start(out=t[:], in_=lp[i].rearrange("(t p) d -> p t d", p=P))
-                elif fam == "oW":
-                    nc.sync.dma_start(out=t[:], in_=oW_v[i])
-                else:
-                    for u in range(2):
-                        nc.sync.dma_start(
-                            out=t[:, 2 * u : 2 * u + 2, :],
-                            in_=vp[i, 256 * u : 256 * u + 256, :].rearrange("(q e) d -> q e d", e=2),
-                        )
-            elif kind == "ms":
-                nc.vector.memset(rows[:].rearrange("p a d -> p (a d)").bitcast(I32), 0)
-                nc.vector.memset(ones[:], 1.0)
-            elif kind == "ldc":
-                for i, vec in enumerate((ob, og, obeta)):
-                    nc.scalar.dma_start(out=rows[0:1, i, :], in_=vec.unsqueeze(0))
-            elif kind == "cmm":
-                t = psc.tile([P, D], BF16, name="c_" + s[1])
-                const[s[1]] = t
-                for nh in range(2):
-                    nc.tensor.matmul(
-                        out=t[:, cols(nh)], lhsT=ones[:], rhs=rows[:, {"og": 1, "be": 2}[s[1]], cols(nh)], start=True, stop=True
-                    )
-            elif kind == "obmm":
-                a = ps2.tile([P, 512], F32, name="obp", tag="s2")
-                acc[("ob", s[1])] = a
-                nc.tensor.matmul(out=a[:], lhsT=ones[:], rhs=rows[:, 0, cols(s[1])], start=True, stop=True)
-            elif kind == "obcp":
-                copy(s[2], const["ob"][:, cols(s[1])], acc[("ob", s[1])][:])
-            elif kind == "ta":
-                b, half = s[1], s[2]
-                xt = ps1.tile([P, 2, 256], F32, name="xt", tag="s1")
-                bank[("ta", b, half)] = xt
-                for u in range(2):
-                    for hh in range(2):
-                        nc.tensor.transpose(
-                            xt[:, u, 128 * hh : 128 * hh + 128],
-                            rawt[("A", b)][:, 2 * half + hh, :].bitcast(F32)[:, 128 * u : 128 * u + 128],
-                            ident[:],
-                        )
-            elif kind == "tacp":
-                b, half = s[1], s[2]
-                if ("AT", b, 0) not in stage:
-                    stage[("AT", b, 0)] = grp.tile([P, 2048], BF16, name="gt", tag="gs", align_bytes=64)
-                g32 = stage[("AT", b, 0)][:].bitcast(F32).rearrange("p (i u) -> p i u", u=2)
-                copy(s[3], g32[:, 256 * half : 256 * half + 256, :], bank[("ta", b, half)][:].rearrange("p u i -> p i u"))
-            elif kind == "reg":
-                fam, i, unit, eng = s[1], s[2], s[3], s[4]
-                g = grp.tile([P, 2048], BF16, name="g" + eng, tag="g" + eng, align_bytes=64)
-                stage[(fam, i, unit)] = g
-                copy(
-                    eng,
-                    g[:].rearrange("p (c i t) -> p c t i", i=4, t=4),
-                    rawt[(fam, i)][:, :, 512 * unit : 512 * unit + 512].rearrange("p t (c i) -> p c t i", i=4),
-                )
-            elif kind == "q":
-                fam, i, unit = s[1], s[2], s[3]
-                w = slice(512 * unit, 512 * unit + 512)
-                nc.vector.quantize_mx(
-                    out=codes[(fam, i)][:, w].bitcast(FP8X4), scales=scales[(fam, i)][:, w], in_=stage[(fam, i, unit)][:]
-                )
-            elif kind == "s1":
-                tau, g = s[1], s[2]
-                b, sg = divmod(tau, 4)
-                wf, rf = ("vp", "AT") if g < 2 else ("lp", "A")
-                bk = ps1.tile([P, 4, 128], F32, name="bank", tag="s1")
-                bank[("s1", tau, g)] = bk
-                for t in range(4):
-                    c0 = 128 * (4 * (g % 2) + t)
-                    nc.tensor.matmul_mx(
-                        out=bk[:, t, :],
-                        lhsT=codes[(wf, b)][:, c0 : c0 + 128].bitcast(FP8X4),
-                        lhsT_scale=scales[(wf, b)][:, c0 : c0 + 128],
-                        rhs=codes[(rf, b)][:, 128 * sg : 128 * sg + 128].bitcast(FP8X4),
-                        rhs_scale=scales[(rf, b)][:, 128 * sg : 128 * sg + 128],
-                        start=True,
-                        stop=True,
-                    )
-            elif kind == "p":
-                tau, g = s[1], s[2]
-                if ("cb", tau) not in stage:
-                    stage[("cb", tau)] = grp.tile([P, 4, 128, 4], BF16, name="gc", tag="gc", align_bytes=64)
-                copy(s[3], stage[("cb", tau)][:, g, :, :], bank[("s1", tau, g)][:].rearrange("p t s -> p s t"))
-            elif kind == "qcb":
-                tau = s[1]
-                cc = cbp.tile([P, 512], U32, name="cb_c", tag="cb_c", align_bytes=64)
-                cs = cbp.tile([P, 512], U8, name="cb_s", tag="cb_s", align_bytes=64)
-                cb[tau] = (cc, cs)
-                nc.vector.quantize_mx(
-                    out=cc[:].bitcast(FP8X4), scales=cs[:], in_=stage[("cb", tau)][:].rearrange("p g s t -> p (g s t)")
-                )
-            elif kind == "s2":
-                tau, nh = s[1], s[2]
-                cc, cs = cb[tau]
-                a = ps2.tile([P, 512], F32, name="acc", tag="s2")
-                acc[(tau, nh)] = a
-                for g in range(4):
-                    nc.tensor.matmul_mx(
-                        out=a[:],
-                        lhsT=cc[:, 128 * g : 128 * g + 128].bitcast(FP8X4),
-                        lhsT_scale=cs[:, 128 * g : 128 * g + 128],
-                        rhs=codes[("oW", g)][:, cols(nh)].bitcast(FP8X4),
-                        rhs_scale=scales[("oW", g)][:, cols(nh)],
-                        start=(g == 0),
-                        stop=(g == 3),
-                    )
-            elif kind == "a":
-                tau, nh = s[1], s[2]
-                if tau not in ht:
-                    ht[tau] = hp.tile([P, D], F32, name="h", tag="h")
-                    small[("sums", tau)] = sm.tile([P, 2], F32, name="sums", tag="sums")
-                nc.vector.scalar_tensor_tensor(
-                    out=ht[tau][:, cols(nh)],
-                    in0=acc[(tau, nh)][:],
-                    scalar=1.0,
-                    in1=const["ob"][:, cols(nh)],
-                    op0=ALU.mult,
-                    op1=ALU.add,
-                    accum_out=small[("sums", tau)][:, nh : nh + 1],
-                )
-            elif kind == "nm":
-                tau = s[1]
-                small[("nm", tau)] = sm.tile([P, 1], F32, name="negmean", tag="negmean")
-                nc.vector.tensor_scalar(
-                    out=small[("nm", tau)][:],
-                    in0=small[("sums", tau)][:, 0:1],
-                    scalar1=small[("sums", tau)][:, 1:2],
-                    scalar2=-1.0 / D,
-                    op0=ALU.add,
-                    op1=ALU.mult,
-                )
-            elif kind == "b":
-                tau = s[1]
-                junk = up.tile([P, D], BF16, name="junk", tag="junk", bufs=1)
-                small[("ssq", tau)] = sm.tile([P, 1], F32, name="ssq", tag="ssq")
-                nc.scalar.activation(
-                    out=junk[:],
-                    in_=ht[tau][:],
-                    func=ACT.Square,
-                    bias=small[("nm", tau)][:, 0:1],
-                    scale=1.0,
-                    accum_out=small[("ssq", tau)][:, 0:1],
-                )
-            elif kind == "sq":
-                tau = s[1]
-                small[("std", tau)] = sm.tile([P, 1], F32, name="std", tag="std")
-                nc.scalar.activation(
-                    out=small[("std", tau)][:], in_=small[("ssq", tau)][:], func=ACT.Sqrt, bias=eps_t[:, 0:1], scale=1.0 / D
-                )
-            elif kind == "rc":
-                tau = s[1]
-                small[("rstd", tau)] = sm.tile([P, 1], F32, name="rstd", tag="rstd")
-                nc.vector.reciprocal(out=small[("rstd", tau)][:], in_=small[("std", tau)][:])
-            elif kind == "c":
-                tau, w = s[1], cols(s[2])
-                if tau not in ut:
-                    ut[tau] = up.tile([P, D], F32, name="u", tag="u")
-                nc.vector.scalar_tensor_tensor(
-                    out=ut[tau][:, w],
-                    in0=ht[tau][:, w],
-                    scalar=small[("nm", tau)][:, 0:1],
-                    in1=const["og"][:, w],
-                    op0=ALU.add,
-                    op1=ALU.mult,
-                )
-            elif kind == "d":
-                tau, w = s[1], cols(s[2])
-                nc.vector.scalar_tensor_tensor(
-                    out=ut[tau][:, w],
-                    in0=ut[tau][:, w],
-                    scalar=small[("rstd", tau)][:, 0:1],
-                    in1=const["be"][:, w],
-                    op0=ALU.mult,
-                    op1=ALU.add,
-                )
-            elif kind == "e":
-                tau, w = s[1], cols(s[2])
-                if s[3] == "v":
-                    nc.vector.tensor_scalar_max(out=ut[tau][:, w], in0=ut[tau][:, w], scalar1=0.0)
-                else:
-                    nc.scalar.activation(out=ut[tau][:, w], in_=ut[tau][:, w], func=ACT.Relu)
+        def load(fam, i):
+            t = raw.tile([P, 4, width[fam]], BF16, name="raw_%s%d" % (fam, i))
+            rawt[(fam, i)] = t
+            if fam == "A":
+                nc.sync.dma_start(out=t[:], in_=A[i].rearrange("(t p) j -> p t j", p=P))
+            elif fam == "lp":
+                nc.sync.dma_start(out=t[:], in_=lp[i].rearrange("(t p) d -> p t d", p=P))
+            elif fam == "oW":
+                nc.sync.dma_start(out=t[:], in_=oW_v[i])
             else:
-                assert kind == "st"
-                tau, w = s[1], cols(s[2])
-                b, sg = divmod(tau, 4)
-                nc.sync.dma_start(out=out[b, 128 * sg : 128 * sg + 128, w], in_=ut[tau][:, w])
+                for u in range(2):
+                    nc.sync.dma_start(
+                        out=t[:, 2 * u : 2 * u + 2, :],
+                        in_=vp[i, 256 * u : 256 * u + 256, :].rearrange("(q e) d -> q e d", e=2),
+                    )
 
-        for s in STEPS:
-            step(s)
+        def spread(dst, row, half):
+            nc.tensor.matmul(out=dst, lhsT=ones[:], rhs=rows[:, row, cols(half)], start=True, stop=True)
+
+        def spread_ob(half):
+            a = ps2.tile([P, 512], F32, name="obp", tag="s2")
+            acc[("ob", half)] = a
+            spread(a[:], 0, half)
+
+        def copy_ob(half):
+            nc.scalar.copy(out=ob_t[:, cols(half)], in_=acc[("ob", half)][:])
+
+        def spread_row(row):
+            t = ps2.tile([P, D], BF16, name="spread", tag="s2")
+            acc[("row", row)] = t
+            for nh in range(2):
+                spread(t[:, cols(nh)], row, nh)
+
+        def copy_row(row):
+            const[row] = keep.tile([P, D], BF16, name="const%d" % row)
+            nc.scalar.copy(out=const[row][:], in_=acc[("row", row)][:])
+
+        def turn(b, half):
+            xt = ps1.tile([P, 2, 256], F32, name="xt", tag="s1")
+            bank[("ta", b, half)] = xt
+            for u in range(2):
+                for hh in range(2):
+                    nc.tensor.transpose(
+                        xt[:, u, 128 * hh : 128 * hh + 128],
+                        rawt[("A", b)][:, 2 * half + hh, :].bitcast(F32)[:, 128 * u : 128 * u + 128],
+                        ident[:],
+                    )
+
+        def turn_copy(b, half):
+            if ("AT", b, 0) not in stage:
+                stage[("AT", b, 0)] = grp.tile([P, 2048], BF16, name="gt", tag="gs", align_bytes=64)
+            g32 = stage[("AT", b, 0)][:].bitcast(F32).rearrange("p (i u) -> p i u", u=2)
+            nc.scalar.copy(out=g32[:, 256 * half : 256 * half + 256, :], in_=bank[("ta", b, half)][:].rearrange("p u i -> p i u"))
+
+        def regroup(fam, i, unit):
+            eng = "v" if (fam, i, unit) in ON_VECTOR else "s"
+            g = grp.tile([P, 2048], BF16, name="g" + eng, tag="g" + eng, align_bytes=64)
+            stage[(fam, i, unit)] = g
+            src = rawt[(fam, i)][:, :, 512 * unit : 512 * unit + 512]
+            copy(eng, g[:].rearrange("p (c i t) -> p c t i", i=4, t=4), src.rearrange("p t (c i) -> p c t i", i=4))
+
+        def piece(fam, i, unit, k):
+            if (fam, i, unit) not in stage:
+                stage[(fam, i, unit)] = grp.tile([P, 2048], BF16, name="gs", tag="gs", align_bytes=64)
+            g = stage[(fam, i, unit)]
+            c0 = 512 * unit + 128 * k
+            copy(
+                "s",
+                g[:, 512 * k : 512 * k + 512].rearrange("p (c i t) -> p c t i", i=4, t=4),
+                rawt[(fam, i)][:, :, c0 : c0 + 128].rearrange("p t (c i) -> p c t i", i=4),
+            )
+
+        def quant(fam, i, unit):
+            w = slice(512 * unit, 512 * unit + 512)
+            nc.vector.quantize_mx(
+                out=codes[(fam, i)][:, w].bitcast(FP8X4), scales=scales[(fam, i)][:, w], in_=stage[(fam, i, unit)][:]
+            )
+
+        def s1(tau, g):
+            b, sg = divmod(tau, 4)
+            wf, rf = ("vp", "AT") if g < 2 else ("lp", "A")
+            bk = ps1.tile([P, 4, 128], F32, name="bank", tag="s1")
+            bank[("s1", tau, g)] = bk
+            for t in range(4):
+                c0 = 128 * (4 * (g % 2) + t)
+                nc.tensor.matmul_mx(
+                    out=bk[:, t, :],
+                    lhsT=codes[(wf, b)][:, c0 : c0 + 128].bitcast(FP8X4),
+                    lhsT_scale=scales[(wf, b)][:, c0 : c0 + 128],
+                    rhs=codes[(rf, b)][:, 128 * sg : 128 * sg + 128].bitcast(FP8X4),
+                    rhs_scale=scales[(rf, b)][:, 128 * sg : 128 * sg + 128],
+                    start=True,
+                    stop=True,
+                )
+
+        def pack(tau, g, eng="s"):
+            if ("cb", tau) not in stage:
+                stage[("cb", tau)] = grp.tile([P, 4, 128, 4], BF16, name="gc", tag="gc", align_bytes=64)
+            copy(eng, stage[("cb", tau)][:, g, :, :], bank[("s1", tau, g)][:].rearrange("p t s -> p s t"))
+
+        def quant_cb(tau):
+            cc = cbp.tile([P, 512], U32, name="cb_c", tag="cb_c", align_bytes=64)
+            cs = cbp.tile([P, 512], U8, name="cb_s", tag="cb_s", align_bytes=64)
+            cb[tau] = (cc, cs)
+            nc.vector.quantize_mx(
+                out=cc[:].bitcast(FP8X4), scales=cs[:], in_=stage[("cb", tau)][:].rearrange("p g s t -> p (g s t)")
+            )
+
+        def s2(tau, nh):
+            cc, cs = cb[tau]
+            a = ps2.tile([P, 512], F32, name="acc", tag="s2")
+            acc[(tau, nh)] = a
+            for g in range(4):
+                nc.tensor.matmul_mx(
+                    out=a[:],
+                    lhsT=cc[:, 128 * g : 128 * g + 128].bitcast(FP8X4),
+                    lhsT_scale=cs[:, 128 * g : 128 * g + 128],
+                    rhs=codes[("oW", g)][:, cols(nh)].bitcast(FP8X4),
+                    rhs_scale=scales[("oW", g)][:, cols(nh)],
+                    start=(g == 0),
+                    stop=(g == 3),
+                )
+
+        def add_ob(tau, nh):
+            if tau not in ht:
+                ht[tau] = hp.tile([P, D], F32, name="h", tag="h")
+                small[("sums", tau)] = sm.tile([P, 2], F32, name="sums", tag="sums")
+            nc.vector.scalar_tensor_tensor(
+                out=ht[tau][:, cols(nh)],
+                in0=acc[(tau, nh)][:],
+                scalar=1.0,
+                in1=ob_t[:, cols(nh)],
+                op0=ALU.mult,
+                op1=ALU.add,
+                accum_out=small[("sums", tau)][:, nh : nh + 1],
+            )
+
+        def neg_mean(tau):
+            small[("nm", tau)] = sm.tile([P, 1], F32, name="negmean", tag="negmean")
+            parts = sm.tile([P, 2], F32, name="parts", tag="parts")
+            nc.scalar.activation(
+                out=parts[:],
+                in_=small[("sums", tau)][:],
+                func=ACT.Identity,
+                scale=-1.0 / D,
+                accum_out=small[("nm", tau)][:],
+            )
+
+        def square(tau):
+            junk = up.tile([P, D], BF16, name="junk", tag="junk", bufs=1)
+            small[("ssq", tau)] = sm.tile([P, 1], F32, name="ssq", tag="ssq")
+            nc.scalar.activation(
+                out=junk[:],
+                in_=ht[tau][:],
+                func=ACT.Square,
+                bias=small[("nm", tau)][:, 0:1],
+                scale=1.0,
+                accum_out=small[("ssq", tau)][:, 0:1],
+            )
+
+        def inverse_std(tau):
+            small[("rstd", tau)] = sm.tile([P, 1], F32, name="rstd", tag="rstd")
+            nc.scalar.activation(
+                out=small[("rstd", tau)][:],
+                in_=small[("ssq", tau)][:],
+                func=ACT.Abs_reciprocal_sqrt,
+                bias=eps_t[:, 0:1],
+                scale=1.0 / D,
+            )
+
+        def gain(tau, nh):
+            w = cols(nh)
+            if tau not in ut:
+                ut[tau] = up.tile([P, D], F32, name="u", tag="u")
+            nc.vector.scalar_tensor_tensor(
+                out=ut[tau][:, w],
+                in0=ht[tau][:, w],
+                scalar=small[("nm", tau)][:, 0:1],
+                in1=const[1][:, w],
+                op0=ALU.add,
+                op1=ALU.mult,
+            )
+
+        def shift_v(tau, nh):
+            w = cols(nh)
+            nc.vector.scalar_tensor_tensor(
+                out=ut[tau][:, w],
+                in0=ut[tau][:, w],
+                scalar=small[("rstd", tau)][:, 0:1],
+                in1=const[2][:, w],
+                op0=ALU.mult,
+                op1=ALU.add,
+            )
+
+        def relu(tau, nh):
+            w = cols(nh)
+            src = ut[tau][:, w]
+            if tau in RELU_V:
+                nc.vector.tensor_scalar_max(out=ut[tau][:, w], in0=src, scalar1=0.0)
+            else:
+                nc.scalar.activation(out=ut[tau][:, w], in_=src, func=ACT.Relu)
+
+        def store(tau, nh):
+            b, sg = divmod(tau, 4)
+            nc.sync.dma_start(out=out[b, 128 * sg : 128 * sg + 128, cols(nh)], in_=ut[tau][:, cols(nh)])
+        nc.vector.memset(rows[:].rearrange("p a d -> p (a d)").bitcast(I32), 0)
+        nc.vector.memset(ones[:], 1.0)
+        for i, vec in enumerate((ob, og, obeta)):
+            nc.scalar.dma_start(out=rows[0:1, i, :], in_=vec.unsqueeze(0))
+
+        call = {
+            "load": load, "turn": turn, "turned": turn_copy, "reg": regroup, "piece": piece, "q": quant,
+            "ob": spread_ob, "obc": copy_ob, "row": spread_row, "s1": s1, "pack": pack, "qcb": quant_cb, "s2": s2, "a": add_ob,
+            "nm": neg_mean, "rowc": copy_row, "b": square, "rs": inverse_std, "c": gain, "d": shift_v, "e": relu, "st": store,
+        }
+        s1_order = [op[1:] for op in TENSOR if op[0] == "s1"]
+        acc_order = [op for op in TENSOR if op[0] in ("ob", "row", "s2", "sp")]
+        turns = [op[1:] for op in TENSOR if op[0] == "turn"]
+        bank_order = [op for op in TENSOR if op[0] in ("s1", "turn")]
+        reg_order = {"v": [], "s": []}
+        for op in VECTOR + SCALAR:
+            if op[0] == "reg" or (op[0] == "piece" and op[4] == 0) or (op[0] == "turned" and op[2] == 0):
+                u = ("AT", op[1], 0) if op[0] == "turned" else op[1:4]
+                reg_order["v" if u in ON_VECTOR else "s"].append(u)
+
+        def freed(op):
+            return ("pack",) + op[1:] if op[0] == "s1" else ("turned",) + op[1:]
+
+        def ring(order, item, depth):
+            k = order.index(item)
+            return order[k - depth] if k >= depth else None
+
+        def needs(op):
+            kind, a = op[0], op[1:]
+            n = []
+            if kind in ("turn", "s1"):
+                old = ring(bank_order, op, N1)
+                if old:
+                    n.append(freed(old))
+            if kind == "turn":
+                n.append(("load", "A", a[0]))
+            elif kind == "turned":
+                n.append(("turn",) + a)
+            elif kind in ("reg", "piece"):
+                n.append(("load",) + a[:2])
+            elif kind == "q":
+                if a[0] == "AT":
+                    n += [("turned", a[1], 0), ("turned", a[1], 1)]
+                elif ("reg",) + a in SCALAR + VECTOR:
+                    n.append(("reg",) + a)
+                else:
+                    n += [("piece",) + a + (k,) for k in range(4)]
+            elif kind == "obc":
+                n.append(("ob", a[0]))
+            elif kind == "s1":
+                b, g = a[0] // 4, a[1]
+                n.append(("q", "vp" if g < 2 else "lp", b, g % 2))
+                n.append(("q", "AT" if g < 2 else "A", b, 0))
+            elif kind == "pack":
+                n.append(("s1",) + a)
+                if a[0] >= 3:
+                    n.append(("qcb", a[0] - 3))
+            elif kind == "qcb":
+                n += [("pack", a[0], g) for g in range(4)]
+                if a[0] >= CB:
+                    n.append(("s2", a[0] - CB, 1))
+            elif kind == "s2":
+                n.append(("qcb", a[0]))
+                n += [("q", "oW", g, a[1]) for g in range(4)]
+            elif kind == "a":
+                n += [("s2",) + a, ("obc", a[1])]
+                if a[0] >= H:
+                    n += [("c", a[0] - H, -1), ("b", a[0] - H)]
+            elif kind == "nm":
+                n += [("a", a[0], 0), ("a", a[0], 1)]
+            elif kind == "b":
+                n.append(("nm", a[0]))
+            elif kind == "rs":
+                n.append(("b", a[0]))
+            elif kind == "c":
+                n += [("nm", a[0]), ("rowc", 1)]
+                if a[0] >= U:
+                    n.append(("st", a[0] - U, -1))
+            elif kind == "d":
+                n += [("rs", a[0]), ("c", a[0], -1) if ("c", a[0], -1) in VECTOR else ("c",) + a, ("rowc", 2)]
+            elif kind == "dg":
+                n.append(("rs", a[0]))
+            elif kind == "sp":
+                n += [("dg", a[0]), ("c", a[0], -1)]
+            elif kind == "rowc":
+                n.append(("row", a[0]))
+            elif kind == "e":
+                n.append((("sp",) if a[0] in PE_SHIFT else ("d",)) + a)
+            elif kind == "st":
+                n += [("e",) + a] if ("e",) + a in SCALAR + VECTOR else [("e", a[0], h) for h in range(2)]
+            if kind in ("ob", "row", "s2", "sp"):
+                old = ring(acc_order, op, N2)
+                if old:
+                    n.append(({"ob": "obc", "row": "rowc", "s2": "a", "sp": "e"}[old[0]],) + old[1:])
+            if kind in ("reg", "piece") or (kind == "turned" and a[1] == 0):
+                u = ("AT", a[0], 0) if kind == "turned" else a[:3]
+                if kind != "piece" or a[3] == 0:
+                    old = ring(reg_order["v" if u in ON_VECTOR else "s"], u, 3)
+                    if old:
+                        n.append(("q",) + old)
+            return n
+
+        done = set()
+        queues = [list(x) for x in (LOADS, TENSOR, VECTOR, SCALAR, GPSIMD, STORES)]
+        while any(queues):
+            before = len(done)
+            for queue in queues:
+                while queue and all(x in done for x in needs(queue[0])):
+                    op = queue.pop(0)
+                    call[op[0]](*op[1:])
+                    done.add(op)
+            assert len(done) > before, [q[0] for q in queues if q]

@@ -22,7 +22,7 @@ H = 4
 U = 4
 N1 = 4
 N2 = 4
-PE_SHIFT = ()
+PE_SHIFT = (4, 6)
 RELU_V = (7,)
 
 
@@ -41,17 +41,17 @@ def tile_clawmatrix_pb_kernel(tc, A, vp, lp, oW, ob, og, obeta, out):
         ctx.enter_context(tc.manual_schedule())
 
         LOADS = [("load", "A", 0), ("load", "vp", 0), ("load", "lp", 0)] + [("load", "oW", g) for g in range(4)]
-        LOADS += [("load", "A", 1), ("load", "vp", 1), ("load", "lp", 1)]
-        OW_S = [("oW", 0, 1), ("oW", 1, 1)]
+        LOADS += [("load", "A", 1), ("load", "vp", 1), ("bc", "ob"), ("load", "lp", 1), ("bc", "og"), ("bc", "be")]
+        OW_S = [("oW", 0, 1), ("oW", 1, 1), ("oW", 2, 1)]
         B1_S = [("vp", 1, 1), ("lp", 1, 1)]
         OW_V = [("oW", g, u) for u in range(2) for g in range(4) if ("oW", g, u) not in OW_S]
         ON_VECTOR = [("A", 0, 0), ("A", 1, 0), ("vp", 0, 0), ("lp", 0, 0), ("vp", 1, 0), ("lp", 1, 0)] + OW_V
         FRONT0 = [(t, g) for t in range(4) for g in range(4)]
         FRONT1 = [(t, g) for t in range(4, 8) for g in range(4)]
 
-        SCALAR = [("turned", 0, 0), ("turned", 0, 1), ("reg", "vp", 0, 1), ("obc", 0), ("obc", 1), ("reg", "lp", 0, 1)]
-        SCALAR += [("reg",) + u for u in OW_S[:2]] + [("pack",) + x for x in FRONT0[:4]]
-        SCALAR += [("pack",) + x for x in FRONT0[4:]] + [("rowc", 1), ("rowc", 2)]
+        SCALAR = [("turned", 0, 0), ("turned", 0, 1), ("reg", "vp", 0, 1), ("reg", "lp", 0, 1)]
+        SCALAR += [("reg",) + u for u in OW_S[:2]] + [("pack",) + x for x in FRONT0[:4]] + [("reg",) + OW_S[2]]
+        SCALAR += [("pack",) + x for x in FRONT0[4:]]
         items = [("turned", 1, 0), ("turned", 1, 1)] + [("piece",) + u + (k,) for u in B1_S for k in range(4)]
         items += [("pack",) + x for x in FRONT1]
         PER = (5, 6, 5, 4, 3, 3, 0, 0, 0, 0)
@@ -63,8 +63,8 @@ def tile_clawmatrix_pb_kernel(tc, A, vp, lp, oW, ob, og, obeta, out):
                 SCALAR += [("nm", r - 1), ("b", r - 1), ("rs", r - 1)]
             SCALAR += mine
             if 1 < r < 9:
-                SCALAR += [("e", r - 2, -1)]
-        GPSIMD = []
+                SCALAR += [("e", r - 2, 0), ("e", r - 2, 1)] if r - 2 in PE_SHIFT else [("e", r - 2, -1)]
+        GPSIMD = [("dg", r) for r in PE_SHIFT]
         STORES = [("st", r, -1) for r in range(7)] + [("st", 7, 0), ("st", 7, 1)]
 
         VECTOR = [("reg", "A", 0, 0), ("q", "A", 0, 0), ("reg", "vp", 0, 0), ("q", "AT", 0, 0), ("q", "vp", 0, 0)]
@@ -72,7 +72,7 @@ def tile_clawmatrix_pb_kernel(tc, A, vp, lp, oW, ob, og, obeta, out):
         ow = [("reg",) + u for u in OW_V]
         oq = [("q",) + u for u in OW_V]
         sq = [("q",) + u for u in OW_S]
-        VECTOR += [ow[0], ("q", "lp", 0, 1), ow[1], oq[0], sq[0], ow[2], oq[1], sq[1], ow[3], oq[2], ow[4], oq[3], ("qcb", 0), ow[5], oq[4], oq[5]]
+        VECTOR += [ow[0], ("q", "lp", 0, 1), ow[1], oq[0], sq[0], ow[2], oq[1], sq[1], ow[3], oq[2], ow[4], oq[3], ("qcb", 0), oq[4], sq[2]]
         VECTOR += [("reg", "A", 1, 0), ("qcb", 1), ("q", "A", 1, 0), ("qcb", 2)]
         FILL = {
             0: [("reg", "vp", 1, 0), ("qcb", 3)],
@@ -86,14 +86,14 @@ def tile_clawmatrix_pb_kernel(tc, A, vp, lp, oW, ob, og, obeta, out):
             f = FILL.get(r, [])
             VECTOR += [("a", r, 0)] if r < 8 else []
             VECTOR += f[:1]
-            VECTOR += [("d", r - 2, -1)] if 1 < r < 9 else []
+            VECTOR += [("d", r - 2, -1)] if 1 < r < 9 and r - 2 not in PE_SHIFT else []
             VECTOR += [("a", r, 1)] if r < 8 else []
             VECTOR += f[1:2]
             VECTOR += [("c", r - 1, -1)] if 0 < r < 9 else []
             VECTOR += f[2:]
         VECTOR += [("d", 7, 0), ("d", 7, 1), ("e", 7, 0), ("e", 7, 1)]
 
-        TENSOR = [("turn", 0, 0), ("turn", 0, 1), ("ob", 0), ("ob", 1), ("row", 1), ("row", 2)]
+        TENSOR = [("turn", 0, 0), ("turn", 0, 1)]
         TENSOR += [("s1",) + x for x in FRONT0] + [("s2", 0, 0), ("s2", 0, 1), ("turn", 1, 0), ("turn", 1, 1)]
         s1s = [("s1",) + x for x in FRONT1]
         sent, packed = 0, 0
@@ -103,6 +103,7 @@ def tile_clawmatrix_pb_kernel(tc, A, vp, lp, oW, ob, og, obeta, out):
             upto = min(16, packed + N1) if packed else 0
             TENSOR += s1s[sent:upto]
             sent = upto
+            TENSOR += [("sp", r - 1, 0), ("sp", r - 1, 1)] if r - 1 in PE_SHIFT else []
 
         eps_t = keep.tile([P, 1], F32, name="eps_t")
         nc.vector.memset(eps_t[:], EPS)
@@ -119,9 +120,7 @@ def tile_clawmatrix_pb_kernel(tc, A, vp, lp, oW, ob, og, obeta, out):
                 codes[(fam, i)] = keep.tile([P, width[fam]], U32, name="%s_c%d" % (fam, i), align_bytes=64)
                 scales[(fam, i)] = keep.tile([P, width[fam]], U8, name="%s_s%d" % (fam, i), align_bytes=64)
         rawt = {}
-        rows = keep.tile([P, 3, D], BF16, name="rows")
-        ones = keep.tile([P, P], BF16, name="ones")
-        ob_t = keep.tile([P, D], F32, name="ob_t")
+        mean16 = keep.tile([P, P], BF16, name="mean16")
         stage = {}
         bank = {}
         cb = {}
@@ -157,26 +156,10 @@ def tile_clawmatrix_pb_kernel(tc, A, vp, lp, oW, ob, og, obeta, out):
                         in_=vp[i, 256 * u : 256 * u + 256, :].rearrange("(q e) d -> q e d", e=2),
                     )
 
-        def spread(dst, row, half):
-            nc.tensor.matmul(out=dst, lhsT=ones[:], rhs=rows[:, row, cols(half)], start=True, stop=True)
-
-        def spread_ob(half):
-            a = ps2.tile([P, 512], F32, name="obp", tag="s2")
-            acc[("ob", half)] = a
-            spread(a[:], 0, half)
-
-        def copy_ob(half):
-            nc.scalar.copy(out=ob_t[:, cols(half)], in_=acc[("ob", half)][:])
-
-        def spread_row(row):
-            t = ps2.tile([P, D], BF16, name="spread", tag="s2")
-            acc[("row", row)] = t
-            for nh in range(2):
-                spread(t[:, cols(nh)], row, nh)
-
-        def copy_row(row):
-            const[row] = keep.tile([P, D], BF16, name="const%d" % row)
-            nc.scalar.copy(out=const[row][:], in_=acc[("row", row)][:])
+        def broadcast(name):
+            const[name] = keep.tile([P, D], BF16, name="row_" + name)
+            vec = {"ob": ob, "og": og, "be": obeta}[name]
+            nc.sync.dma_start(out=const[name][:], in_=vec.partition_broadcast(P))
 
         def turn(b, half):
             xt = ps1.tile([P, 2, 256], F32, name="xt", tag="s1")
@@ -272,7 +255,7 @@ def tile_clawmatrix_pb_kernel(tc, A, vp, lp, oW, ob, og, obeta, out):
                 out=ht[tau][:, cols(nh)],
                 in0=acc[(tau, nh)][:],
                 scalar=1.0,
-                in1=ob_t[:, cols(nh)],
+                in1=const["ob"][:, cols(nh)],
                 op0=ALU.mult,
                 op1=ALU.add,
                 accum_out=small[("sums", tau)][:, nh : nh + 1],
@@ -319,10 +302,27 @@ def tile_clawmatrix_pb_kernel(tc, A, vp, lp, oW, ob, og, obeta, out):
                 out=ut[tau][:, w],
                 in0=ht[tau][:, w],
                 scalar=small[("nm", tau)][:, 0:1],
-                in1=const[1][:, w],
+                in1=const["og"][:, w],
                 op0=ALU.add,
                 op1=ALU.mult,
             )
+
+        def diagonal(tau):
+            small[("diag", tau)] = sm.tile([P, P], F32, name="diag", tag="diag", bufs=2)
+            nc.gpsimd.tensor_scalar(
+                out=small[("diag", tau)][:],
+                in0=ident[:],
+                scalar1=small[("rstd", tau)][:, 0:1],
+                scalar2=0.0,
+                op0=ALU.mult,
+                op1=ALU.add,
+            )
+
+        def shift_pe(tau, nh):
+            po = ps2.tile([P, 512], F32, name="po", tag="s2")
+            acc[("sp", tau, nh)] = po
+            nc.tensor.matmul(out=po[:], lhsT=mean16[:], rhs=const["be"][:, cols(nh)], start=True, stop=False)
+            nc.tensor.matmul(out=po[:], lhsT=small[("diag", tau)][:], rhs=ut[tau][:, cols(nh)], start=False, stop=True)
 
         def shift_v(tau, nh):
             w = cols(nh)
@@ -330,14 +330,14 @@ def tile_clawmatrix_pb_kernel(tc, A, vp, lp, oW, ob, og, obeta, out):
                 out=ut[tau][:, w],
                 in0=ut[tau][:, w],
                 scalar=small[("rstd", tau)][:, 0:1],
-                in1=const[2][:, w],
+                in1=const["be"][:, w],
                 op0=ALU.mult,
                 op1=ALU.add,
             )
 
         def relu(tau, nh):
             w = cols(nh)
-            src = ut[tau][:, w]
+            src = acc[("sp", tau, nh)][:] if tau in PE_SHIFT else ut[tau][:, w]
             if tau in RELU_V:
                 nc.vector.tensor_scalar_max(out=ut[tau][:, w], in0=src, scalar1=0.0)
             else:
@@ -346,18 +346,15 @@ def tile_clawmatrix_pb_kernel(tc, A, vp, lp, oW, ob, og, obeta, out):
         def store(tau, nh):
             b, sg = divmod(tau, 4)
             nc.sync.dma_start(out=out[b, 128 * sg : 128 * sg + 128, cols(nh)], in_=ut[tau][:, cols(nh)])
-        nc.vector.memset(rows[:].rearrange("p a d -> p (a d)").bitcast(I32), 0)
-        nc.vector.memset(ones[:], 1.0)
-        for i, vec in enumerate((ob, og, obeta)):
-            nc.scalar.dma_start(out=rows[0:1, i, :], in_=vec.unsqueeze(0))
+        nc.vector.memset(mean16[:], 1.0 / P)
 
         call = {
             "load": load, "turn": turn, "turned": turn_copy, "reg": regroup, "piece": piece, "q": quant,
-            "ob": spread_ob, "obc": copy_ob, "row": spread_row, "s1": s1, "pack": pack, "qcb": quant_cb, "s2": s2, "a": add_ob,
-            "nm": neg_mean, "rowc": copy_row, "b": square, "rs": inverse_std, "c": gain, "d": shift_v, "e": relu, "st": store,
+            "bc": broadcast, "s1": s1, "pack": pack, "qcb": quant_cb, "s2": s2, "a": add_ob,
+            "nm": neg_mean, "dg": diagonal, "sp": shift_pe, "b": square, "rs": inverse_std, "c": gain, "d": shift_v, "e": relu, "st": store,
         }
         s1_order = [op[1:] for op in TENSOR if op[0] == "s1"]
-        acc_order = [op for op in TENSOR if op[0] in ("ob", "row", "s2", "sp")]
+        acc_order = [op for op in TENSOR if op[0] in ("s2", "sp")]
         turns = [op[1:] for op in TENSOR if op[0] == "turn"]
         bank_order = [op for op in TENSOR if op[0] in ("s1", "turn")]
         reg_order = {"v": [], "s": []}
@@ -393,8 +390,6 @@ def tile_clawmatrix_pb_kernel(tc, A, vp, lp, oW, ob, og, obeta, out):
                     n.append(("reg",) + a)
                 else:
                     n += [("piece",) + a + (k,) for k in range(4)]
-            elif kind == "obc":
-                n.append(("ob", a[0]))
             elif kind == "s1":
                 b, g = a[0] // 4, a[1]
                 n.append(("q", "vp" if g < 2 else "lp", b, g % 2))
@@ -411,7 +406,7 @@ def tile_clawmatrix_pb_kernel(tc, A, vp, lp, oW, ob, og, obeta, out):
                 n.append(("qcb", a[0]))
                 n += [("q", "oW", g, a[1]) for g in range(4)]
             elif kind == "a":
-                n += [("s2",) + a, ("obc", a[1])]
+                n += [("s2",) + a, ("bc", "ob")]
                 if a[0] >= H:
                     n += [("c", a[0] - H, -1), ("b", a[0] - H)]
             elif kind == "nm":
@@ -421,25 +416,23 @@ def tile_clawmatrix_pb_kernel(tc, A, vp, lp, oW, ob, og, obeta, out):
             elif kind == "rs":
                 n.append(("b", a[0]))
             elif kind == "c":
-                n += [("nm", a[0]), ("rowc", 1)]
+                n += [("nm", a[0]), ("bc", "og")]
                 if a[0] >= U:
                     n.append(("st", a[0] - U, -1))
             elif kind == "d":
-                n += [("rs", a[0]), ("c", a[0], -1) if ("c", a[0], -1) in VECTOR else ("c",) + a, ("rowc", 2)]
+                n += [("rs", a[0]), ("c", a[0], -1) if ("c", a[0], -1) in VECTOR else ("c",) + a, ("bc", "be")]
             elif kind == "dg":
                 n.append(("rs", a[0]))
             elif kind == "sp":
-                n += [("dg", a[0]), ("c", a[0], -1)]
-            elif kind == "rowc":
-                n.append(("row", a[0]))
+                n += [("dg", a[0]), ("c", a[0], -1), ("bc", "be")]
             elif kind == "e":
                 n.append((("sp",) if a[0] in PE_SHIFT else ("d",)) + a)
             elif kind == "st":
                 n += [("e",) + a] if ("e",) + a in SCALAR + VECTOR else [("e", a[0], h) for h in range(2)]
-            if kind in ("ob", "row", "s2", "sp"):
+            if kind in ("s2", "sp"):
                 old = ring(acc_order, op, N2)
                 if old:
-                    n.append(({"ob": "obc", "row": "rowc", "s2": "a", "sp": "e"}[old[0]],) + old[1:])
+                    n.append(({"s2": "a", "sp": "e"}[old[0]],) + old[1:])
             if kind in ("reg", "piece") or (kind == "turned" and a[1] == 0):
                 u = ("AT", a[0], 0) if kind == "turned" else a[:3]
                 if kind != "piece" or a[3] == 0:

@@ -22,8 +22,8 @@ H = 4
 U = 4
 N1 = 4
 N2 = 4
-PE_SHIFT = (4, 6)
-RELU_V = (7,)
+PE_SHIFT = (5,)
+RELU_V = ((7, 1),)
 
 
 def tile_clawmatrix_pb_kernel(tc, A, vp, lp, oW, ob, og, obeta, out):
@@ -59,11 +59,10 @@ def tile_clawmatrix_pb_kernel(tc, A, vp, lp, oW, ob, og, obeta, out):
         for r in range(10):
             mine, items = items[: PER[r]], items[PER[r] :]
             MINE.append(mine)
-            if 0 < r < 9:
-                SCALAR += [("nm", r - 1), ("b", r - 1), ("rs", r - 1)]
-            SCALAR += mine
+            SCALAR += [("b", r - 1)] + mine[:1] + [("rs", r - 1)] + mine[1:] if 0 < r < 9 else mine
             if 1 < r < 9:
                 SCALAR += [("e", r - 2, 0), ("e", r - 2, 1)] if r - 2 in PE_SHIFT else [("e", r - 2, -1)]
+        SCALAR += [("e", 7, 0)]
         GPSIMD = [("dg", r) for r in PE_SHIFT]
         STORES = [("st", r, -1) for r in range(7)] + [("st", 7, 0), ("st", 7, 1)]
 
@@ -90,8 +89,9 @@ def tile_clawmatrix_pb_kernel(tc, A, vp, lp, oW, ob, og, obeta, out):
             VECTOR += [("a", r, 1)] if r < 8 else []
             VECTOR += f[1:2]
             VECTOR += [("c", r - 1, -1)] if 0 < r < 9 else []
+            VECTOR += [("nm", r)] if r < 8 else []
             VECTOR += f[2:]
-        VECTOR += [("d", 7, 0), ("d", 7, 1), ("e", 7, 0), ("e", 7, 1)]
+        VECTOR += [("d", 7, 0), ("d", 7, 1), ("e", 7, 1)]
 
         TENSOR = [("turn", 0, 0), ("turn", 0, 1)]
         TENSOR += [("s1",) + x for x in FRONT0] + [("s2", 0, 0), ("s2", 0, 1), ("turn", 1, 0), ("turn", 1, 1)]
@@ -143,17 +143,14 @@ def tile_clawmatrix_pb_kernel(tc, A, vp, lp, oW, ob, og, obeta, out):
         def load(fam, i):
             t = raw.tile([P, 4, width[fam]], BF16, name="raw_%s%d" % (fam, i))
             rawt[(fam, i)] = t
-            if fam == "A":
-                nc.sync.dma_start(out=t[:], in_=A[i].rearrange("(t p) j -> p t j", p=P))
-            elif fam == "lp":
-                nc.sync.dma_start(out=t[:], in_=lp[i].rearrange("(t p) d -> p t d", p=P))
-            elif fam == "oW":
+            if fam == "oW":
                 nc.sync.dma_start(out=t[:], in_=oW_v[i])
             else:
+                src = {"A": A, "vp": vp, "lp": lp}[fam]
                 for u in range(2):
                     nc.sync.dma_start(
                         out=t[:, 2 * u : 2 * u + 2, :],
-                        in_=vp[i, 256 * u : 256 * u + 256, :].rearrange("(q e) d -> q e d", e=2),
+                        in_=src[i, 256 * u : 256 * u + 256, :].rearrange("(q e) d -> q e d", e=2),
                     )
 
         def broadcast(name):
@@ -176,7 +173,10 @@ def tile_clawmatrix_pb_kernel(tc, A, vp, lp, oW, ob, og, obeta, out):
             if ("AT", b, 0) not in stage:
                 stage[("AT", b, 0)] = grp.tile([P, 2048], BF16, name="gt", tag="gs", align_bytes=64)
             g32 = stage[("AT", b, 0)][:].bitcast(F32).rearrange("p (i u) -> p i u", u=2)
-            nc.scalar.copy(out=g32[:, 256 * half : 256 * half + 256, :], in_=bank[("ta", b, half)][:].rearrange("p u i -> p i u"))
+            nc.scalar.copy(
+                out=g32[:, 256 * half : 256 * half + 256, :].rearrange("p (q e) w -> p q e w", e=2),
+                in_=bank[("ta", b, half)][:].rearrange("p w (e q) -> p q e w", e=2),
+            )
 
         def regroup(fam, i, unit):
             eng = "v" if (fam, i, unit) in ON_VECTOR else "s"
@@ -263,13 +263,13 @@ def tile_clawmatrix_pb_kernel(tc, A, vp, lp, oW, ob, og, obeta, out):
 
         def neg_mean(tau):
             small[("nm", tau)] = sm.tile([P, 1], F32, name="negmean", tag="negmean")
-            parts = sm.tile([P, 2], F32, name="parts", tag="parts")
-            nc.scalar.activation(
-                out=parts[:],
-                in_=small[("sums", tau)][:],
-                func=ACT.Identity,
-                scale=-1.0 / D,
-                accum_out=small[("nm", tau)][:],
+            nc.vector.tensor_scalar(
+                out=small[("nm", tau)][:],
+                in0=small[("sums", tau)][:, 0:1],
+                scalar1=small[("sums", tau)][:, 1:2],
+                scalar2=-1.0 / D,
+                op0=ALU.add,
+                op1=ALU.mult,
             )
 
         def square(tau):
@@ -338,7 +338,7 @@ def tile_clawmatrix_pb_kernel(tc, A, vp, lp, oW, ob, og, obeta, out):
         def relu(tau, nh):
             w = cols(nh)
             src = acc[("sp", tau, nh)][:] if tau in PE_SHIFT else ut[tau][:, w]
-            if tau in RELU_V:
+            if (tau, nh) in RELU_V:
                 nc.vector.tensor_scalar_max(out=ut[tau][:, w], in0=src, scalar1=0.0)
             else:
                 nc.scalar.activation(out=ut[tau][:, w], in_=src, func=ACT.Relu)

@@ -18,12 +18,15 @@ EPS = 1e-5
 FLOPS = 2 * (2 * B * S * S * D) + 2 * (B * S) * (2 * D) * D
 TILES = 8
 CB = 4
-H = 4
-U = 4
+RUN = 8
+H = 5
+U = 5
+LB = 2
+LD = 3
 N1 = 4
 N2 = 4
 PE_SHIFT = (5,)
-RELU_V = ((7, 1),)
+RELU_V = ((6, -1), (7, 0), (7, 1))
 
 
 def tile_clawmatrix_pb_kernel(tc, A, vp, lp, oW, ob, og, obeta, out):
@@ -46,23 +49,31 @@ def tile_clawmatrix_pb_kernel(tc, A, vp, lp, oW, ob, og, obeta, out):
         B1_S = [("vp", 1, 1), ("lp", 1, 1)]
         OW_V = [("oW", g, u) for u in range(2) for g in range(4) if ("oW", g, u) not in OW_S]
         ON_VECTOR = [("A", 0, 0), ("A", 1, 0), ("vp", 0, 0), ("lp", 0, 0), ("vp", 1, 0), ("lp", 1, 0)] + OW_V
+        BR = [t + 1 for t in range(8)]
+        DR = [min(t + 3, 8) for t in range(8)]
         FRONT0 = [(t, g) for t in range(4) for g in range(4)]
         FRONT1 = [(t, g) for t in range(4, 8) for g in range(4)]
 
         SCALAR = [("turned", 0, 0), ("turned", 0, 1), ("reg", "vp", 0, 1), ("reg", "lp", 0, 1)]
         SCALAR += [("reg",) + u for u in OW_S[:2]] + [("pack",) + x for x in FRONT0[:4]] + [("reg",) + OW_S[2]]
         SCALAR += [("pack",) + x for x in FRONT0[4:]]
-        items = [("turned", 1, 0), ("turned", 1, 1)] + [("piece",) + u + (k,) for u in B1_S for k in range(4)]
+        items = [("piece",) + B1_S[0] + (k,) for k in range(4)] + [("turned", 1, 0), ("turned", 1, 1)] + [("piece",) + B1_S[1] + (k,) for k in range(4)]
         items += [("pack",) + x for x in FRONT1]
-        PER = (5, 6, 5, 4, 3, 3, 0, 0, 0, 0)
+        PER = (5, 7, 5, 4, 3, 2, 0, 0, 0, 0)
         MINE = []
         for r in range(10):
             mine, items = items[: PER[r]], items[PER[r] :]
             MINE.append(mine)
-            SCALAR += [("b", r - 1)] + mine[:1] + [("rs", r - 1)] + mine[1:] if 0 < r < 9 else mine
-            if 1 < r < 9:
-                SCALAR += [("e", r - 2, 0), ("e", r - 2, 1)] if r - 2 in PE_SHIFT else [("e", r - 2, -1)]
-        SCALAR += [("e", 7, 0)]
+            done_b = [t for t in range(8) if BR[t] == r]
+            done_e = [t for t in range(6) if DR[t] == r]
+            seq = []
+            for t in done_b:
+                seq += [("b", t)] + mine[:1]
+                mine = mine[1:]
+                seq += [("rs", t)]
+            SCALAR += seq + mine
+            for t in done_e:
+                SCALAR += [("e", t, 0), ("e", t, 1)] if t in PE_SHIFT else [("e", t, -1)]
         GPSIMD = [("dg", r) for r in PE_SHIFT]
         STORES = [("st", r, -1) for r in range(7)] + [("st", 7, 0), ("st", 7, 1)]
 
@@ -74,8 +85,8 @@ def tile_clawmatrix_pb_kernel(tc, A, vp, lp, oW, ob, og, obeta, out):
         VECTOR += [ow[0], ("q", "lp", 0, 1), ow[1], oq[0], sq[0], ow[2], oq[1], sq[1], ow[3], oq[2], ow[4], oq[3], ("qcb", 0), oq[4], sq[2]]
         VECTOR += [("reg", "A", 1, 0), ("qcb", 1), ("q", "A", 1, 0), ("qcb", 2)]
         FILL = {
-            0: [("reg", "vp", 1, 0), ("qcb", 3)],
-            1: [("q", "AT", 1, 0), ("reg", "lp", 1, 0), ("q", "vp", 1, 0), ("q", "vp", 1, 1), ("q", "lp", 1, 0), ("q", "lp", 1, 1)],
+            0: [("reg", "vp", 1, 0), ("qcb", 3), ("q", "vp", 1, 0), ("reg", "lp", 1, 0)],
+            1: [("q", "vp", 1, 1), ("q", "AT", 1, 0), ("q", "lp", 1, 0), ("q", "lp", 1, 1)],
             3: [("qcb", 4)],
             4: [("qcb", 5)],
             5: [("qcb", 6)],
@@ -85,13 +96,13 @@ def tile_clawmatrix_pb_kernel(tc, A, vp, lp, oW, ob, og, obeta, out):
             f = FILL.get(r, [])
             VECTOR += [("a", r, 0)] if r < 8 else []
             VECTOR += f[:1]
-            VECTOR += [("d", r - 2, -1)] if 1 < r < 9 and r - 2 not in PE_SHIFT else []
+            VECTOR += [("d", t, -1) for t in range(7) if DR[t] == r and t not in PE_SHIFT]
             VECTOR += [("a", r, 1)] if r < 8 else []
             VECTOR += f[1:2]
             VECTOR += [("c", r - 1, -1)] if 0 < r < 9 else []
             VECTOR += [("nm", r)] if r < 8 else []
             VECTOR += f[2:]
-        VECTOR += [("d", 7, 0), ("d", 7, 1), ("e", 7, 1)]
+        VECTOR += [("e", 6, -1), ("d", 7, 0), ("d", 7, 1), ("e", 7, 0), ("e", 7, 1)]
 
         TENSOR = [("turn", 0, 0), ("turn", 0, 1)]
         TENSOR += [("s1",) + x for x in FRONT0] + [("s2", 0, 0), ("s2", 0, 1), ("turn", 1, 0), ("turn", 1, 1)]
@@ -103,7 +114,8 @@ def tile_clawmatrix_pb_kernel(tc, A, vp, lp, oW, ob, og, obeta, out):
             upto = min(16, packed + N1) if packed else 0
             TENSOR += s1s[sent:upto]
             sent = upto
-            TENSOR += [("sp", r - 1, 0), ("sp", r - 1, 1)] if r - 1 in PE_SHIFT else []
+            TENSOR += [("sp", t, h) for t in PE_SHIFT if BR[t] == r for h in range(2)]
+        TENSOR += [("sp", t, h) for t in PE_SHIFT if BR[t] == 8 for h in range(2)]
 
         eps_t = keep.tile([P, 1], F32, name="eps_t")
         nc.vector.memset(eps_t[:], EPS)
@@ -183,7 +195,7 @@ def tile_clawmatrix_pb_kernel(tc, A, vp, lp, oW, ob, og, obeta, out):
             g = grp.tile([P, 2048], BF16, name="g" + eng, tag="g" + eng, align_bytes=64)
             stage[(fam, i, unit)] = g
             src = rawt[(fam, i)][:, :, 512 * unit : 512 * unit + 512]
-            copy(eng, g[:].rearrange("p (c i t) -> p c t i", i=4, t=4), src.rearrange("p t (c i) -> p c t i", i=4))
+            copy(eng, g[:].rearrange("p (c i t) -> p c t i", i=RUN, t=4), src.rearrange("p t (c i) -> p c t i", i=RUN))
 
         def piece(fam, i, unit, k):
             if (fam, i, unit) not in stage:
@@ -192,8 +204,8 @@ def tile_clawmatrix_pb_kernel(tc, A, vp, lp, oW, ob, og, obeta, out):
             c0 = 512 * unit + 128 * k
             copy(
                 "s",
-                g[:, 512 * k : 512 * k + 512].rearrange("p (c i t) -> p c t i", i=4, t=4),
-                rawt[(fam, i)][:, :, c0 : c0 + 128].rearrange("p t (c i) -> p c t i", i=4),
+                g[:, 512 * k : 512 * k + 512].rearrange("p (c i t) -> p c t i", i=RUN, t=4),
+                rawt[(fam, i)][:, :, c0 : c0 + 128].rearrange("p t (c i) -> p c t i", i=RUN),
             )
 
         def quant(fam, i, unit):

@@ -18,14 +18,11 @@ EPS = 1e-5
 FLOPS = 2 * (2 * B * S * S * D) + 2 * (B * S) * (2 * D) * D
 TILES = 8
 CB = 4
-RUN = 8
 H = 5
 U = 5
-LB = 2
-LD = 3
 N1 = 4
-N2 = 4
-PE_SHIFT = (5,)
+N2 = 8 - N1
+PE_SHIFT = (4,)
 RELU_V = ((6, -1), (7, 0), (7, 1))
 
 
@@ -49,8 +46,9 @@ def tile_clawmatrix_pb_kernel(tc, A, vp, lp, oW, ob, og, obeta, out):
         B1_S = [("vp", 1, 1), ("lp", 1, 1)]
         OW_V = [("oW", g, u) for u in range(2) for g in range(4) if ("oW", g, u) not in OW_S]
         ON_VECTOR = [("A", 0, 0), ("A", 1, 0), ("vp", 0, 0), ("lp", 0, 0), ("vp", 1, 0), ("lp", 1, 0)] + OW_V
-        BR = [t + 1 for t in range(8)]
-        DR = [min(t + 3, 8) for t in range(8)]
+        BR = [min(t + 1, 8) if t < 4 else min(t + 1, 8) for t in range(8)]
+        DR = [min(t + 3, 9) for t in range(8)]
+        CR = [min(t + 1, 8) for t in range(8)]
         FRONT0 = [(t, g) for t in range(4) for g in range(4)]
         FRONT1 = [(t, g) for t in range(4, 8) for g in range(4)]
 
@@ -59,21 +57,28 @@ def tile_clawmatrix_pb_kernel(tc, A, vp, lp, oW, ob, og, obeta, out):
         SCALAR += [("pack",) + x for x in FRONT0[4:]]
         items = [("piece",) + B1_S[0] + (k,) for k in range(4)] + [("turned", 1, 0), ("turned", 1, 1)] + [("piece",) + B1_S[1] + (k,) for k in range(4)]
         items += [("pack",) + x for x in FRONT1]
-        PER = (5, 7, 5, 4, 3, 2, 0, 0, 0, 0)
+        PER = (5, 6, 5, 4, 4, 2, 0, 0, 0, 0)
         MINE = []
         for r in range(10):
             mine, items = items[: PER[r]], items[PER[r] :]
             MINE.append(mine)
             done_b = [t for t in range(8) if BR[t] == r]
-            done_e = [t for t in range(6) if DR[t] == r]
-            seq = []
+            done_e = [t for t in range(6) if min(DR[t] + (1 if t < 3 else 0), 9) == r]
+            seq, mine = mine[:3], mine[3:]
             for t in done_b:
                 seq += [("b", t)] + mine[:1]
+                if not mine and done_e:
+                    x = done_e.pop(0)
+                    seq += [("e", x, 0), ("e", x, 1)] if x in PE_SHIFT else [("e", x, -1)]
                 mine = mine[1:]
                 seq += [("rs", t)]
-            SCALAR += seq + mine
+            SCALAR += seq
+            if not False:
+                SCALAR += mine
+                mine = []
             for t in done_e:
                 SCALAR += [("e", t, 0), ("e", t, 1)] if t in PE_SHIFT else [("e", t, -1)]
+            SCALAR += mine
         GPSIMD = [("dg", r) for r in PE_SHIFT]
         STORES = [("st", r, -1) for r in range(7)] + [("st", 7, 0), ("st", 7, 1)]
 
@@ -82,11 +87,11 @@ def tile_clawmatrix_pb_kernel(tc, A, vp, lp, oW, ob, og, obeta, out):
         ow = [("reg",) + u for u in OW_V]
         oq = [("q",) + u for u in OW_V]
         sq = [("q",) + u for u in OW_S]
-        VECTOR += [ow[0], ("q", "lp", 0, 1), ow[1], oq[0], sq[0], ow[2], oq[1], sq[1], ow[3], oq[2], ow[4], oq[3], ("qcb", 0), oq[4], sq[2]]
-        VECTOR += [("reg", "A", 1, 0), ("qcb", 1), ("q", "A", 1, 0), ("qcb", 2)]
+        VECTOR += [ow[0], ("q", "lp", 0, 1), ow[1], oq[0], sq[0], ow[2], oq[1], sq[1], ow[3], oq[2], ow[4], oq[3], ("qcb", 0), oq[4], sq[2], ("reg", "A", 1, 0), ("qcb", 1), ("q", "A", 1, 0), ("qcb", 2)]
         FILL = {
             0: [("reg", "vp", 1, 0), ("qcb", 3), ("q", "vp", 1, 0), ("reg", "lp", 1, 0)],
             1: [("q", "vp", 1, 1), ("q", "AT", 1, 0), ("q", "lp", 1, 0), ("q", "lp", 1, 1)],
+            2: [],
             3: [("qcb", 4)],
             4: [("qcb", 5)],
             5: [("qcb", 6)],
@@ -96,16 +101,19 @@ def tile_clawmatrix_pb_kernel(tc, A, vp, lp, oW, ob, og, obeta, out):
             f = FILL.get(r, [])
             VECTOR += [("a", r, 0)] if r < 8 else []
             VECTOR += f[:1]
-            VECTOR += [("d", t, -1) for t in range(7) if DR[t] == r and t not in PE_SHIFT]
+            VECTOR += [("d", t, -1) for t in range(7) if DR[t] == r and t not in PE_SHIFT] if True else []
             VECTOR += [("a", r, 1)] if r < 8 else []
+            VECTOR += [("d", t, -1) for t in range(7) if DR[t] == r and t not in PE_SHIFT] if not True else []
             VECTOR += f[1:2]
-            VECTOR += [("c", r - 1, -1)] if 0 < r < 9 else []
-            VECTOR += [("nm", r)] if r < 8 else []
+            VECTOR += [("nm", r)] if r < 8 and False else []
+            VECTOR += [("c", t, -1) for t in range(8) if CR[t] == r]
+            VECTOR += [("nm", r)] if r < 8 and not False else []
             VECTOR += f[2:]
         VECTOR += [("e", 6, -1), ("d", 7, 0), ("d", 7, 1), ("e", 7, 0), ("e", 7, 1)]
 
+
         TENSOR = [("turn", 0, 0), ("turn", 0, 1)]
-        TENSOR += [("s1",) + x for x in FRONT0] + [("s2", 0, 0), ("s2", 0, 1), ("turn", 1, 0), ("turn", 1, 1)]
+        TENSOR += [("s1",) + x for x in FRONT0[:14]] + [("s2", 0, 0)] + [("s1",) + x for x in FRONT0[14:]] + [("s2", 0, 1), ("turn", 1, 0), ("turn", 1, 1)]
         s1s = [("s1",) + x for x in FRONT1]
         sent, packed = 0, 0
         for r in range(8):
@@ -114,8 +122,8 @@ def tile_clawmatrix_pb_kernel(tc, A, vp, lp, oW, ob, og, obeta, out):
             upto = min(16, packed + N1) if packed else 0
             TENSOR += s1s[sent:upto]
             sent = upto
-            TENSOR += [("sp", t, h) for t in PE_SHIFT if BR[t] == r for h in range(2)]
-        TENSOR += [("sp", t, h) for t in PE_SHIFT if BR[t] == 8 for h in range(2)]
+            TENSOR += [("sp", t, h) for t in PE_SHIFT if max(BR[t], CR[t]) + 1 == r for h in range(2)]
+        TENSOR += [("sp", t, h) for t in PE_SHIFT if max(BR[t], CR[t]) + 1 >= 8 for h in range(2)]
 
         eps_t = keep.tile([P, 1], F32, name="eps_t")
         nc.vector.memset(eps_t[:], EPS)
@@ -195,7 +203,7 @@ def tile_clawmatrix_pb_kernel(tc, A, vp, lp, oW, ob, og, obeta, out):
             g = grp.tile([P, 2048], BF16, name="g" + eng, tag="g" + eng, align_bytes=64)
             stage[(fam, i, unit)] = g
             src = rawt[(fam, i)][:, :, 512 * unit : 512 * unit + 512]
-            copy(eng, g[:].rearrange("p (c i t) -> p c t i", i=RUN, t=4), src.rearrange("p t (c i) -> p c t i", i=RUN))
+            copy(eng, g[:].rearrange("p (c i t) -> p c t i", i=4, t=4), src.rearrange("p t (c i) -> p c t i", i=4))
 
         def piece(fam, i, unit, k):
             if (fam, i, unit) not in stage:
@@ -204,8 +212,8 @@ def tile_clawmatrix_pb_kernel(tc, A, vp, lp, oW, ob, og, obeta, out):
             c0 = 512 * unit + 128 * k
             copy(
                 "s",
-                g[:, 512 * k : 512 * k + 512].rearrange("p (c i t) -> p c t i", i=RUN, t=4),
-                rawt[(fam, i)][:, :, c0 : c0 + 128].rearrange("p t (c i) -> p c t i", i=RUN),
+                g[:, 512 * k : 512 * k + 512].rearrange("p (c i t) -> p c t i", i=4, t=4),
+                rawt[(fam, i)][:, :, c0 : c0 + 128].rearrange("p t (c i) -> p c t i", i=4),
             )
 
         def quant(fam, i, unit):

@@ -21,9 +21,10 @@ CB = 4
 H = 5
 U = 5
 N1 = 4
-N2 = 8 - N1
-PE_SHIFT = (4,)
-RELU_V = ((6, -1), (7, 0), (7, 1))
+N2 = 4
+PE_SHIFT = (3, 5)
+RELU_V = ((6, 1), (7, 0), (7, 1))
+NM_ON_SCALAR = True
 
 
 def tile_clawmatrix_pb_kernel(tc, A, vp, lp, oW, ob, og, obeta, out):
@@ -42,56 +43,54 @@ def tile_clawmatrix_pb_kernel(tc, A, vp, lp, oW, ob, og, obeta, out):
 
         LOADS = [("load", "A", 0), ("load", "vp", 0), ("load", "lp", 0)] + [("load", "oW", g) for g in range(4)]
         LOADS += [("load", "A", 1), ("load", "vp", 1), ("bc", "ob"), ("load", "lp", 1), ("bc", "og"), ("bc", "be")]
-        OW_S = [("oW", 0, 1), ("oW", 1, 1), ("oW", 2, 1)]
-        B1_S = [("vp", 1, 1), ("lp", 1, 1)]
-        OW_V = [("oW", g, u) for u in range(2) for g in range(4) if ("oW", g, u) not in OW_S]
-        ON_VECTOR = [("A", 0, 0), ("A", 1, 0), ("vp", 0, 0), ("lp", 0, 0), ("vp", 1, 0), ("lp", 1, 0)] + OW_V
-        BR = [min(t + 1, 8) if t < 4 else min(t + 1, 8) for t in range(8)]
-        DR = [min(t + 3, 9) for t in range(8)]
-        CR = [min(t + 1, 8) for t in range(8)]
+        BR = [t + 1 for t in range(8)]
+        DR = [min(t + 3, 8) for t in range(8)]
         FRONT0 = [(t, g) for t in range(4) for g in range(4)]
         FRONT1 = [(t, g) for t in range(4, 8) for g in range(4)]
 
-        SCALAR = [("turned", 0, 0), ("turned", 0, 1), ("reg", "vp", 0, 1), ("reg", "lp", 0, 1)]
-        SCALAR += [("reg",) + u for u in OW_S[:2]] + [("pack",) + x for x in FRONT0[:4]] + [("reg",) + OW_S[2]]
-        SCALAR += [("pack",) + x for x in FRONT0[4:]]
-        items = [("piece",) + B1_S[0] + (k,) for k in range(4)] + [("turned", 1, 0), ("turned", 1, 1)] + [("piece",) + B1_S[1] + (k,) for k in range(4)]
-        items += [("pack",) + x for x in FRONT1]
+
+        def left(fam, i):
+            return [("vs", fam, i, 0, 512)]
+
+
+        def right(fam, i, cuts=1):
+            w = 512 // cuts
+            return [("ss", fam, i, 512 + w * k, 512 + w * (k + 1)) for k in range(cuts)]
+
+
+        SCALAR = [("turned", 0, 0), ("turned", 0, 1)] + right("vp", 0) + right("lp", 0) + right("oW", 0) + right("oW", 1)
+        SCALAR += [("pack",) + x for x in FRONT0[:4]] + right("oW", 2) + [("pack",) + x for x in FRONT0[4:]]
+        items = right("vp", 1, 4) + [("turned", 1, 0), ("turned", 1, 1)] + right("lp", 1, 4) + [("pack",) + x for x in FRONT1]
         PER = (5, 6, 5, 4, 4, 2, 0, 0, 0, 0)
         MINE = []
         for r in range(10):
             mine, items = items[: PER[r]], items[PER[r] :]
             MINE.append(mine)
-            done_b = [t for t in range(8) if BR[t] == r]
             done_e = [t for t in range(6) if min(DR[t] + (1 if t < 3 else 0), 9) == r]
-            seq, mine = mine[:3], mine[3:]
-            for t in done_b:
-                seq += [("b", t)] + mine[:1]
-                if not mine and done_e:
+            if 0 < r < 9:
+                t = r - 1
+                if NM_ON_SCALAR:
+                    SCALAR += mine[:1] + [("nm", t)] + mine[1:3] + [("b", t)] + mine[3:4]
+                else:
+                    SCALAR += mine[:3] + [("b", t)] + mine[3:4]
+                if len(mine) < 4 and done_e:
                     x = done_e.pop(0)
-                    seq += [("e", x, 0), ("e", x, 1)] if x in PE_SHIFT else [("e", x, -1)]
-                mine = mine[1:]
-                seq += [("rs", t)]
-            SCALAR += seq
-            if not False:
+                    SCALAR += [("e", x, 0), ("e", x, 1)] if x in PE_SHIFT else [("e", x, -1)]
+                SCALAR += [("rs", t)] + mine[4:]
+            else:
                 SCALAR += mine
-                mine = []
-            for t in done_e:
-                SCALAR += [("e", t, 0), ("e", t, 1)] if t in PE_SHIFT else [("e", t, -1)]
-            SCALAR += mine
+            for x in done_e:
+                SCALAR += [("e", x, 0), ("e", x, 1)] if x in PE_SHIFT else [("e", x, -1)]
+        SCALAR += [("e", 6, 0)]
         GPSIMD = [("dg", r) for r in PE_SHIFT]
         STORES = [("st", r, -1) for r in range(7)] + [("st", 7, 0), ("st", 7, 1)]
 
-        VECTOR = [("reg", "A", 0, 0), ("q", "A", 0, 0), ("reg", "vp", 0, 0), ("q", "AT", 0, 0), ("q", "vp", 0, 0)]
-        VECTOR += [("reg", "lp", 0, 0), ("q", "vp", 0, 1), ("q", "lp", 0, 0)]
-        ow = [("reg",) + u for u in OW_V]
-        oq = [("q",) + u for u in OW_V]
-        sq = [("q",) + u for u in OW_S]
-        VECTOR += [ow[0], ("q", "lp", 0, 1), ow[1], oq[0], sq[0], ow[2], oq[1], sq[1], ow[3], oq[2], ow[4], oq[3], ("qcb", 0), oq[4], sq[2], ("reg", "A", 1, 0), ("qcb", 1), ("q", "A", 1, 0), ("qcb", 2)]
+        VECTOR = [("vs", "A", 0, 0, 512), ("q", "A", 0)] + left("vp", 0) + [("q", "AT", 0)] + left("lp", 0) + [("q", "vp", 0)] + left("oW", 0) + [("q", "lp", 0)]
+        VECTOR += left("oW", 1) + [("q", "oW", 0)] + left("oW", 2) + [("q", "oW", 1), ("vs", "oW", 3, 0, 1024), ("qcb", 0), ("q", "oW", 2)]
+        VECTOR += [("vs", "A", 1, 0, 512), ("q", "oW", 3), ("qcb", 1), ("q", "A", 1), ("qcb", 2)]
         FILL = {
-            0: [("reg", "vp", 1, 0), ("qcb", 3), ("q", "vp", 1, 0), ("reg", "lp", 1, 0)],
-            1: [("q", "vp", 1, 1), ("q", "AT", 1, 0), ("q", "lp", 1, 0), ("q", "lp", 1, 1)],
-            2: [],
+            0: left("vp", 1) + [("qcb", 3)] + left("lp", 1),
+            1: [("q", "vp", 1), ("q", "AT", 1), ("q", "lp", 1)],
             3: [("qcb", 4)],
             4: [("qcb", 5)],
             5: [("qcb", 6)],
@@ -101,16 +100,13 @@ def tile_clawmatrix_pb_kernel(tc, A, vp, lp, oW, ob, og, obeta, out):
             f = FILL.get(r, [])
             VECTOR += [("a", r, 0)] if r < 8 else []
             VECTOR += f[:1]
-            VECTOR += [("d", t, -1) for t in range(7) if DR[t] == r and t not in PE_SHIFT] if True else []
+            VECTOR += [("d", t, -1) for t in range(7) if DR[t] == r and t not in PE_SHIFT]
             VECTOR += [("a", r, 1)] if r < 8 else []
-            VECTOR += [("d", t, -1) for t in range(7) if DR[t] == r and t not in PE_SHIFT] if not True else []
             VECTOR += f[1:2]
-            VECTOR += [("nm", r)] if r < 8 and False else []
-            VECTOR += [("c", t, -1) for t in range(8) if CR[t] == r]
-            VECTOR += [("nm", r)] if r < 8 and not False else []
+            VECTOR += [("c", r - 1, -1)] if 0 < r < 9 else []
+            VECTOR += [("nm", r)] if r < 8 and not NM_ON_SCALAR else []
             VECTOR += f[2:]
-        VECTOR += [("e", 6, -1), ("d", 7, 0), ("d", 7, 1), ("e", 7, 0), ("e", 7, 1)]
-
+        VECTOR += [("e", 6, 1), ("d", 7, 0), ("d", 7, 1), ("e", 7, 0), ("e", 7, 1)]
 
         TENSOR = [("turn", 0, 0), ("turn", 0, 1)]
         TENSOR += [("s1",) + x for x in FRONT0[:14]] + [("s2", 0, 0)] + [("s1",) + x for x in FRONT0[14:]] + [("s2", 0, 1), ("turn", 1, 0), ("turn", 1, 1)]
@@ -122,8 +118,8 @@ def tile_clawmatrix_pb_kernel(tc, A, vp, lp, oW, ob, og, obeta, out):
             upto = min(16, packed + N1) if packed else 0
             TENSOR += s1s[sent:upto]
             sent = upto
-            TENSOR += [("sp", t, h) for t in PE_SHIFT if max(BR[t], CR[t]) + 1 == r for h in range(2)]
-        TENSOR += [("sp", t, h) for t in PE_SHIFT if max(BR[t], CR[t]) + 1 >= 8 for h in range(2)]
+            TENSOR += [("sp", t, h) for t in PE_SHIFT if t + 2 == r for h in range(2)]
+        TENSOR += [("sp", t, h) for t in PE_SHIFT if t + 2 >= 8 for h in range(2)]
 
         eps_t = keep.tile([P, 1], F32, name="eps_t")
         nc.vector.memset(eps_t[:], EPS)
@@ -152,6 +148,8 @@ def tile_clawmatrix_pb_kernel(tc, A, vp, lp, oW, ob, og, obeta, out):
         oW_v = oW.rearrange("(g t p) n -> g p t n", t=4, p=P)
 
         def cols(half):
+            if half > 1:
+                return slice(256 * half, 256 * half + 256)
             return slice(0, D) if half < 0 else slice(512 * half, 512 * half + 512)
 
         def copy(eng, dst, src):
@@ -190,36 +188,32 @@ def tile_clawmatrix_pb_kernel(tc, A, vp, lp, oW, ob, og, obeta, out):
                     )
 
         def turn_copy(b, half):
-            if ("AT", b, 0) not in stage:
-                stage[("AT", b, 0)] = grp.tile([P, 2048], BF16, name="gt", tag="gs", align_bytes=64)
-            g32 = stage[("AT", b, 0)][:].bitcast(F32).rearrange("p (i u) -> p i u", u=2)
+            if ("AT", b) not in stage:
+                stage[("AT", b)] = grp.tile([P, 4 * S], BF16, name="g", tag="gA", align_bytes=64)
+            g32 = stage[("AT", b)][:].bitcast(F32).rearrange("p (i u) -> p i u", u=2)
             nc.scalar.copy(
                 out=g32[:, 256 * half : 256 * half + 256, :].rearrange("p (q e) w -> p q e w", e=2),
                 in_=bank[("ta", b, half)][:].rearrange("p w (e q) -> p q e w", e=2),
             )
 
-        def regroup(fam, i, unit):
-            eng = "v" if (fam, i, unit) in ON_VECTOR else "s"
-            g = grp.tile([P, 2048], BF16, name="g" + eng, tag="g" + eng, align_bytes=64)
-            stage[(fam, i, unit)] = g
-            src = rawt[(fam, i)][:, :, 512 * unit : 512 * unit + 512]
-            copy(eng, g[:].rearrange("p (c i t) -> p c t i", i=4, t=4), src.rearrange("p t (c i) -> p c t i", i=4))
-
-        def piece(fam, i, unit, k):
-            if (fam, i, unit) not in stage:
-                stage[(fam, i, unit)] = grp.tile([P, 2048], BF16, name="gs", tag="gs", align_bytes=64)
-            g = stage[(fam, i, unit)]
-            c0 = 512 * unit + 128 * k
+        def group(eng, fam, i, c0, c1):
+            if (fam, i) not in stage:
+                stage[(fam, i)] = grp.tile([P, 4 * width[fam]], BF16, name="g", tag="gA" if fam == "A" else "gB", align_bytes=64)
             copy(
-                "s",
-                g[:, 512 * k : 512 * k + 512].rearrange("p (c i t) -> p c t i", i=4, t=4),
-                rawt[(fam, i)][:, :, c0 : c0 + 128].rearrange("p t (c i) -> p c t i", i=4),
+                eng,
+                stage[(fam, i)][:, 4 * c0 : 4 * c1].rearrange("p (c i t) -> p c t i", i=4, t=4),
+                rawt[(fam, i)][:, :, c0:c1].rearrange("p t (c i) -> p c t i", i=4),
             )
 
-        def quant(fam, i, unit):
-            w = slice(512 * unit, 512 * unit + 512)
+        def group_v(fam, i, c0, c1):
+            group("v", fam, i, c0, c1)
+
+        def group_s(fam, i, c0, c1):
+            group("s", fam, i, c0, c1)
+
+        def quant(fam, i):
             nc.vector.quantize_mx(
-                out=codes[(fam, i)][:, w].bitcast(FP8X4), scales=scales[(fam, i)][:, w], in_=stage[(fam, i, unit)][:]
+                out=codes[(fam, i)][:].bitcast(FP8X4), scales=scales[(fam, i)][:], in_=stage[(fam, i)][:]
             )
 
         def s1(tau, g):
@@ -283,13 +277,13 @@ def tile_clawmatrix_pb_kernel(tc, A, vp, lp, oW, ob, og, obeta, out):
 
         def neg_mean(tau):
             small[("nm", tau)] = sm.tile([P, 1], F32, name="negmean", tag="negmean")
-            nc.vector.tensor_scalar(
-                out=small[("nm", tau)][:],
-                in0=small[("sums", tau)][:, 0:1],
-                scalar1=small[("sums", tau)][:, 1:2],
-                scalar2=-1.0 / D,
-                op0=ALU.add,
-                op1=ALU.mult,
+            parts = sm.tile([P, 2], F32, name="parts", tag="parts")
+            nc.scalar.activation(
+                out=parts[:],
+                in_=small[("sums", tau)][:],
+                func=ACT.Identity,
+                scale=-1.0 / D,
+                accum_out=small[("nm", tau)][:],
             )
 
         def square(tau):
@@ -369,96 +363,71 @@ def tile_clawmatrix_pb_kernel(tc, A, vp, lp, oW, ob, og, obeta, out):
         nc.vector.memset(mean16[:], 1.0 / P)
 
         call = {
-            "load": load, "turn": turn, "turned": turn_copy, "reg": regroup, "piece": piece, "q": quant,
+            "load": load, "turn": turn, "turned": turn_copy, "vs": group_v, "ss": group_s, "q": quant,
             "bc": broadcast, "s1": s1, "pack": pack, "qcb": quant_cb, "s2": s2, "a": add_ob,
             "nm": neg_mean, "dg": diagonal, "sp": shift_pe, "b": square, "rs": inverse_std, "c": gain, "d": shift_v, "e": relu, "st": store,
         }
-        s1_order = [op[1:] for op in TENSOR if op[0] == "s1"]
-        acc_order = [op for op in TENSOR if op[0] in ("s2", "sp")]
-        turns = [op[1:] for op in TENSOR if op[0] == "turn"]
-        bank_order = [op for op in TENSOR if op[0] in ("s1", "turn")]
-        reg_order = {"v": [], "s": []}
-        for op in VECTOR + SCALAR:
-            if op[0] == "reg" or (op[0] == "piece" and op[4] == 0) or (op[0] == "turned" and op[2] == 0):
-                u = ("AT", op[1], 0) if op[0] == "turned" else op[1:4]
-                reg_order["v" if u in ON_VECTOR else "s"].append(u)
 
-        def freed(op):
-            return ("pack",) + op[1:] if op[0] == "s1" else ("turned",) + op[1:]
+        bank_order = [op for op in TENSOR if op[0] in ("s1", "turn")]
+        acc_order = [op for op in TENSOR if op[0] in ("s2", "sp")]
+        small_order = [x for b in range(2) for x in (("A", b), ("AT", b))]
+        big_order = [op[1:] for op in LOADS if op[0] == "load" and op[1] != "A"]
+        parts_of = {}
+        for op in VECTOR + SCALAR:
+            if op[0] in ("vs", "ss"):
+                parts_of.setdefault(op[1:3], []).append(op)
 
         def ring(order, item, depth):
             k = order.index(item)
-            return order[k - depth] if k >= depth else None
+            return [order[k - depth]] if k >= depth else []
 
         def needs(op):
             kind, a = op[0], op[1:]
             n = []
             if kind in ("turn", "s1"):
-                old = ring(bank_order, op, N1)
-                if old:
-                    n.append(freed(old))
+                n += [(("pack",) if x[0] == "s1" else ("turned",)) + x[1:] for x in ring(bank_order, op, N1)]
+            if kind in ("s2", "sp"):
+                n += [(("a",) if x[0] == "s2" else ("e",)) + x[1:] for x in ring(acc_order, op, N2)]
             if kind == "turn":
-                n.append(("load", "A", a[0]))
+                n += [("load", "A", a[0])]
             elif kind == "turned":
-                n.append(("turn",) + a)
-            elif kind in ("reg", "piece"):
-                n.append(("load",) + a[:2])
+                n += [("turn",) + a] + [("q",) + x for x in ring(small_order, ("AT", a[0]), 3)]
+            elif kind in ("vs", "ss"):
+                n += [("load",) + a[:2]]
+                n += [("q",) + x for x in (ring(small_order, a[:2], 3) if a[0] == "A" else ring(big_order, a[:2], 3))]
             elif kind == "q":
                 if a[0] == "AT":
                     n += [("turned", a[1], 0), ("turned", a[1], 1)]
-                elif ("reg",) + a in SCALAR + VECTOR:
-                    n.append(("reg",) + a)
                 else:
-                    n += [("piece",) + a + (k,) for k in range(4)]
+                    n += parts_of[a]
             elif kind == "s1":
-                b, g = a[0] // 4, a[1]
-                n.append(("q", "vp" if g < 2 else "lp", b, g % 2))
-                n.append(("q", "AT" if g < 2 else "A", b, 0))
+                n += [("q", "vp" if a[1] < 2 else "lp", a[0] // 4), ("q", "AT" if a[1] < 2 else "A", a[0] // 4)]
             elif kind == "pack":
-                n.append(("s1",) + a)
-                if a[0] >= 3:
-                    n.append(("qcb", a[0] - 3))
+                n += [("s1",) + a] + ([("qcb", a[0] - 3)] if a[0] >= 3 else [])
             elif kind == "qcb":
-                n += [("pack", a[0], g) for g in range(4)]
-                if a[0] >= CB:
-                    n.append(("s2", a[0] - CB, 1))
+                n += [("pack", a[0], g) for g in range(4)] + ([("s2", a[0] - CB, 1)] if a[0] >= CB else [])
             elif kind == "s2":
-                n.append(("qcb", a[0]))
-                n += [("q", "oW", g, a[1]) for g in range(4)]
+                n += [("qcb", a[0])] + [("q", "oW", g) for g in range(4)]
             elif kind == "a":
-                n += [("s2",) + a, ("bc", "ob")]
-                if a[0] >= H:
-                    n += [("c", a[0] - H, -1), ("b", a[0] - H)]
+                n += [("s2",) + a, ("bc", "ob")] + ([("c", a[0] - H, -1), ("b", a[0] - H)] if a[0] >= H else [])
             elif kind == "nm":
                 n += [("a", a[0], 0), ("a", a[0], 1)]
             elif kind == "b":
-                n.append(("nm", a[0]))
+                n += [("nm", a[0])]
             elif kind == "rs":
-                n.append(("b", a[0]))
+                n += [("b", a[0])]
             elif kind == "c":
-                n += [("nm", a[0]), ("bc", "og")]
-                if a[0] >= U:
-                    n.append(("st", a[0] - U, -1))
-            elif kind == "d":
-                n += [("rs", a[0]), ("c", a[0], -1) if ("c", a[0], -1) in VECTOR else ("c",) + a, ("bc", "be")]
+                n += [("nm", a[0]), ("bc", "og")] + ([("st", a[0] - U, -1)] if a[0] >= U else [])
             elif kind == "dg":
-                n.append(("rs", a[0]))
+                n += [("rs", a[0])]
+            elif kind == "d":
+                n += [("rs", a[0]), ("c", a[0], -1), ("bc", "be")]
             elif kind == "sp":
                 n += [("dg", a[0]), ("c", a[0], -1), ("bc", "be")]
             elif kind == "e":
-                n.append((("sp",) if a[0] in PE_SHIFT else ("d",)) + a)
+                n += [("sp",) + a if a[0] in PE_SHIFT else ("d", a[0], -1 if a[0] < 7 else min(a[1], 1))]
             elif kind == "st":
                 n += [("e",) + a] if ("e",) + a in SCALAR + VECTOR else [("e", a[0], h) for h in range(2)]
-            if kind in ("s2", "sp"):
-                old = ring(acc_order, op, N2)
-                if old:
-                    n.append(({"s2": "a", "sp": "e"}[old[0]],) + old[1:])
-            if kind in ("reg", "piece") or (kind == "turned" and a[1] == 0):
-                u = ("AT", a[0], 0) if kind == "turned" else a[:3]
-                if kind != "piece" or a[3] == 0:
-                    old = ring(reg_order["v" if u in ON_VECTOR else "s"], u, 3)
-                    if old:
-                        n.append(("q",) + old)
             return n
 
         done = set()

@@ -18,6 +18,7 @@ EPS = 1e-5
 FLOPS = 2 * (2 * B * S * S * D) + 2 * (B * S) * (2 * D) * D
 TILES = 8
 CB = 4
+RUN = 8
 H = 5
 U = 5
 N1 = 4
@@ -201,8 +202,8 @@ def tile_clawmatrix_pb_kernel(tc, A, vp, lp, oW, ob, og, obeta, out):
                 stage[(fam, i)] = grp.tile([P, 4 * width[fam]], BF16, name="g", tag="gA" if fam == "A" else "gB", align_bytes=64)
             copy(
                 eng,
-                stage[(fam, i)][:, 4 * c0 : 4 * c1].rearrange("p (c i t) -> p c t i", i=4, t=4),
-                rawt[(fam, i)][:, :, c0:c1].rearrange("p t (c i) -> p c t i", i=4),
+                stage[(fam, i)][:, 4 * c0 : 4 * c1].rearrange("p (c i t) -> p c t i", i=RUN, t=4),
+                rawt[(fam, i)][:, :, c0:c1].rearrange("p t (c i) -> p c t i", i=RUN),
             )
 
         def group_v(fam, i, c0, c1):

from contextlib import ExitStack

import concourse.mybir as mybir
from concourse.masks import make_identity

F32 = mybir.dt.float32
BF16 = mybir.dt.bfloat16
U32 = mybir.dt.uint32
U8 = mybir.dt.uint8
I32 = mybir.dt.int32
FP8X4 = mybir.dt.float8_e4m3fn_x4
ALU = mybir.AluOpType
ACT = mybir.ActivationFunctionType

P = 128
B, S, D = 2, 512, 1024
EPS = 1e-5
FLOPS = 2 * (2 * B * S * S * D) + 2 * (B * S) * (2 * D) * D
TILES = 8
CB = 4
RUN = 8
H = 5
U = 5
N1 = 4
N2 = 4
PE_SHIFT = (3, 5)
RELU_V = ((6, 1), (7, 0), (7, 1))
NM_ON_SCALAR = True


def tile_clawmatrix_pb_kernel(tc, A, vp, lp, oW, ob, og, obeta, out):
    nc = tc.nc
    with ExitStack() as ctx:
        raw = ctx.enter_context(tc.tile_pool(name="raw", bufs=1))
        grp = ctx.enter_context(tc.tile_pool(name="grp", bufs=3))
        keep = ctx.enter_context(tc.tile_pool(name="keep", bufs=1))
        cbp = ctx.enter_context(tc.tile_pool(name="cbp", bufs=CB))
        hp = ctx.enter_context(tc.tile_pool(name="hp", bufs=H))
        up = ctx.enter_context(tc.tile_pool(name="up", bufs=U))
        sm = ctx.enter_context(tc.tile_pool(name="sm", bufs=8))
        ps1 = ctx.enter_context(tc.psum_pool(name="ps1", bufs=N1))
        ps2 = ctx.enter_context(tc.psum_pool(name="ps2", bufs=N2))
        ctx.enter_context(tc.manual_schedule())

        LOADS = [("load", "A", 0), ("load", "vp", 0), ("load", "lp", 0)] + [("load", "oW", g) for g in range(4)]
        LOADS += [("load", "A", 1), ("load", "vp", 1), ("bc", "ob"), ("load", "lp", 1), ("bc", "og"), ("bc", "be")]
        BR = [t + 1 for t in range(8)]
        DR = [min(t + 3, 8) for t in range(8)]
        FRONT0 = [(t, g) for t in range(4) for g in range(4)]
        FRONT1 = [(t, g) for t in range(4, 8) for g in range(4)]


        def left(fam, i):
            return [("vs", fam, i, 0, 512)]


        def right(fam, i, cuts=1):
            w = 512 // cuts
            return [("ss", fam, i, 512 + w * k, 512 + w * (k + 1)) for k in range(cuts)]


        SCALAR = [("turned", 0, 0), ("turned", 0, 1)] + right("vp", 0) + right("lp", 0) + right("oW", 0) + right("oW", 1)
        SCALAR += [("pack",) + x for x in FRONT0[:4]] + right("oW", 2) + [("pack",) + x for x in FRONT0[4:]]
        items = right("vp", 1, 4) + [("turned", 1, 0), ("turned", 1, 1)] + right("lp", 1, 4) + [("pack",) + x for x in FRONT1]
        PER = (5, 6, 5, 4, 4, 2, 0, 0, 0, 0)
        MINE = []
        for r in range(10):
            mine, items = items[: PER[r]], items[PER[r] :]
            MINE.append(mine)
            done_e = [t for t in range(6) if min(DR[t] + (1 if t < 3 else 0), 9) == r]
            if 0 < r < 9:
                t = r - 1
                if NM_ON_SCALAR:
                    SCALAR += mine[:1] + [("nm", t)] + mine[1:3] + [("b", t)] + mine[3:4]
                else:
                    SCALAR += mine[:3] + [("b", t)] + mine[3:4]
                if len(mine) < 4 and done_e:
                    x = done_e.pop(0)
                    SCALAR += [("e", x, 0), ("e", x, 1)] if x in PE_SHIFT else [("e", x, -1)]
                SCALAR += [("rs", t)] + mine[4:]
            else:
                SCALAR += mine
            for x in done_e:
                SCALAR += [("e", x, 0), ("e", x, 1)] if x in PE_SHIFT else [("e", x, -1)]
        SCALAR += [("e", 6, 0)]
        GPSIMD = [("dg", r) for r in PE_SHIFT]
        STORES = [("st", r, -1) for r in range(7)] + [("st", 7, 0), ("st", 7, 1)]

        VECTOR = [("vs", "A", 0, 0, 512), ("q", "A", 0)] + left("vp", 0) + [("q", "AT", 0)] + left("lp", 0) + [("q", "vp", 0)] + left("oW", 0) + [("q", "lp", 0)]
        VECTOR += left("oW", 1) + [("q", "oW", 0)] + left("oW", 2) + [("q", "oW", 1), ("vs", "oW", 3, 0, 1024), ("qcb", 0), ("q", "oW", 2)]
        VECTOR += [("vs", "A", 1, 0, 512), ("q", "oW", 3), ("qcb", 1), ("q", "A", 1), ("qcb", 2)]
        FILL = {
            0: left("vp", 1) + [("qcb", 3)] + left("lp", 1),
            1: [("q", "vp", 1), ("q", "AT", 1), ("q", "lp", 1)],
            3: [("qcb", 4)],
            4: [("qcb", 5)],
            5: [("qcb", 6)],
            6: [("qcb", 7)],
        }
        for r in range(10):
            f = FILL.get(r, [])
            VECTOR += [("a", r, 0)] if r < 8 else []
            VECTOR += f[:1]
            VECTOR += [("d", t, -1) for t in range(7) if DR[t] == r and t not in PE_SHIFT]
            VECTOR += [("a", r, 1)] if r < 8 else []
            VECTOR += f[1:2]
            VECTOR += [("c", r - 1, -1)] if 0 < r < 9 else []
            VECTOR += [("nm", r)] if r < 8 and not NM_ON_SCALAR else []
            VECTOR += f[2:]
        VECTOR += [("e", 6, 1), ("d", 7, 0), ("d", 7, 1), ("e", 7, 0), ("e", 7, 1)]

        TENSOR = [("turn", 0, 0), ("turn", 0, 1)]
        TENSOR += [("s1",) + x for x in FRONT0[:14]] + [("s2", 0, 0)] + [("s1",) + x for x in FRONT0[14:]] + [("s2", 0, 1), ("turn", 1, 0), ("turn", 1, 1)]
        s1s = [("s1",) + x for x in FRONT1]
        sent, packed = 0, 0
        for r in range(8):
            TENSOR += [("s2", r + 1, 0), ("s2", r + 1, 1)] if r < 7 else []
            packed += len([x for x in MINE[r] if x[0] == "pack"])
            upto = min(16, packed + N1) if packed else 0
            TENSOR += s1s[sent:upto]
            sent = upto
            TENSOR += [("sp", t, h) for t in PE_SHIFT if t + 2 == r for h in range(2)]
        TENSOR += [("sp", t, h) for t in PE_SHIFT if t + 2 >= 8 for h in range(2)]

        eps_t = keep.tile([P, 1], F32, name="eps_t")
        nc.vector.memset(eps_t[:], EPS)
        warm = keep.tile([P, 1], F32, name="warm")
        nc.scalar.activation(out=warm[:], in_=eps_t[:], func=ACT.Abs_reciprocal_sqrt)
        ident = keep.tile([P, P], F32, name="ident")
        make_identity(nc, ident[:])

        width = {"A": S, "AT": S, "vp": D, "lp": D, "oW": D}
        codes = {}
        scales = {}
        for fam, count in (("A", 2), ("AT", 2), ("vp", 2), ("lp", 2), ("oW", 4)):
            for i in range(count):
                codes[(fam, i)] = keep.tile([P, width[fam]], U32, name="%s_c%d" % (fam, i), align_bytes=64)
                scales[(fam, i)] = keep.tile([P, width[fam]], U8, name="%s_s%d" % (fam, i), align_bytes=64)
        rawt = {}
        mean16 = keep.tile([P, P], BF16, name="mean16")
        stage = {}
        bank = {}
        cb = {}
        acc = {}
        ht = {}
        ut = {}
        small = {}
        const = {}
        oW_v = oW.rearrange("(g t p) n -> g p t n", t=4, p=P)

        def cols(half):
            if half > 1:
                return slice(256 * half, 256 * half + 256)
            return slice(0, D) if half < 0 else slice(512 * half, 512 * half + 512)

        def copy(eng, dst, src):
            if eng == "v":
                nc.vector.tensor_copy(out=dst, in_=src)
            else:
                nc.scalar.copy(out=dst, in_=src)

        def load(fam, i):
            t = raw.tile([P, 4, width[fam]], BF16, name="raw_%s%d" % (fam, i))
            rawt[(fam, i)] = t
            if fam == "oW":
                nc.sync.dma_start(out=t[:], in_=oW_v[i])
            else:
                src = {"A": A, "vp": vp, "lp": lp}[fam]
                for u in range(2):
                    nc.sync.dma_start(
                        out=t[:, 2 * u : 2 * u + 2, :],
                        in_=src[i, 256 * u : 256 * u + 256, :].rearrange("(q e) d -> q e d", e=2),
                    )

        def broadcast(name):
            const[name] = keep.tile([P, D], BF16, name="row_" + name)
            vec = {"ob": ob, "og": og, "be": obeta}[name]
            nc.sync.dma_start(out=const[name][:], in_=vec.partition_broadcast(P))

        def turn(b, half):
            xt = ps1.tile([P, 2, 256], F32, name="xt", tag="s1")
            bank[("ta", b, half)] = xt
            for u in range(2):
                for hh in range(2):
                    nc.tensor.transpose(
                        xt[:, u, 128 * hh : 128 * hh + 128],
                        rawt[("A", b)][:, 2 * half + hh, :].bitcast(F32)[:, 128 * u : 128 * u + 128],
                        ident[:],
                    )

        def turn_copy(b, half):
            if ("AT", b) not in stage:
                stage[("AT", b)] = grp.tile([P, 4 * S], BF16, name="g", tag="gA", align_bytes=64)
            g32 = stage[("AT", b)][:].bitcast(F32).rearrange("p (i u) -> p i u", u=2)
            nc.scalar.copy(
                out=g32[:, 256 * half : 256 * half + 256, :].rearrange("p (q e) w -> p q e w", e=2),
                in_=bank[("ta", b, half)][:].rearrange("p w (e q) -> p q e w", e=2),
            )

        def group(eng, fam, i, c0, c1):
            if (fam, i) not in stage:
                stage[(fam, i)] = grp.tile([P, 4 * width[fam]], BF16, name="g", tag="gA" if fam == "A" else "gB", align_bytes=64)
            copy(
                eng,
                stage[(fam, i)][:, 4 * c0 : 4 * c1].rearrange("p (c i t) -> p c t i", i=RUN, t=4),
                rawt[(fam, i)][:, :, c0:c1].rearrange("p t (c i) -> p c t i", i=RUN),
            )

        def group_v(fam, i, c0, c1):
            group("v", fam, i, c0, c1)

        def group_s(fam, i, c0, c1):
            group("s", fam, i, c0, c1)

        def quant(fam, i):
            nc.vector.quantize_mx(
                out=codes[(fam, i)][:].bitcast(FP8X4), scales=scales[(fam, i)][:], in_=stage[(fam, i)][:]
            )

        def s1(tau, g):
            b, sg = divmod(tau, 4)
            wf, rf = ("vp", "AT") if g < 2 else ("lp", "A")
            bk = ps1.tile([P, 4, 128], F32, name="bank", tag="s1")
            bank[("s1", tau, g)] = bk
            for t in range(4):
                c0 = 128 * (4 * (g % 2) + t)
                nc.tensor.matmul_mx(
                    out=bk[:, t, :],
                    lhsT=codes[(wf, b)][:, c0 : c0 + 128].bitcast(FP8X4),
                    lhsT_scale=scales[(wf, b)][:, c0 : c0 + 128],
                    rhs=codes[(rf, b)][:, 128 * sg : 128 * sg + 128].bitcast(FP8X4),
                    rhs_scale=scales[(rf, b)][:, 128 * sg : 128 * sg + 128],
                    start=True,
                    stop=True,
                )

        def pack(tau, g, eng="s"):
            if ("cb", tau) not in stage:
                stage[("cb", tau)] = grp.tile([P, 4, 128, 4], BF16, name="gc", tag="gc", align_bytes=64)
            copy(eng, stage[("cb", tau)][:, g, :, :], bank[("s1", tau, g)][:].rearrange("p t s -> p s t"))

        def quant_cb(tau):
            cc = cbp.tile([P, 512], U32, name="cb_c", tag="cb_c", align_bytes=64)
            cs = cbp.tile([P, 512], U8, name="cb_s", tag="cb_s", align_bytes=64)
            cb[tau] = (cc, cs)
            nc.vector.quantize_mx(
                out=cc[:].bitcast(FP8X4), scales=cs[:], in_=stage[("cb", tau)][:].rearrange("p g s t -> p (g s t)")
            )

        def s2(tau, nh):
            cc, cs = cb[tau]
            a = ps2.tile([P, 512], F32, name="acc", tag="s2")
            acc[(tau, nh)] = a
            for g in range(4):
                nc.tensor.matmul_mx(
                    out=a[:],
                    lhsT=cc[:, 128 * g : 128 * g + 128].bitcast(FP8X4),
                    lhsT_scale=cs[:, 128 * g : 128 * g + 128],
                    rhs=codes[("oW", g)][:, cols(nh)].bitcast(FP8X4),
                    rhs_scale=scales[("oW", g)][:, cols(nh)],
                    start=(g == 0),
                    stop=(g == 3),
                )

        def add_ob(tau, nh):
            if tau not in ht:
                ht[tau] = hp.tile([P, D], F32, name="h", tag="h")
                small[("sums", tau)] = sm.tile([P, 2], F32, name="sums", tag="sums")
            nc.vector.scalar_tensor_tensor(
                out=ht[tau][:, cols(nh)],
                in0=acc[(tau, nh)][:],
                scalar=1.0,
                in1=const["ob"][:, cols(nh)],
                op0=ALU.mult,
                op1=ALU.add,
                accum_out=small[("sums", tau)][:, nh : nh + 1],
            )

        def neg_mean(tau):
            small[("nm", tau)] = sm.tile([P, 1], F32, name="negmean", tag="negmean")
            parts = sm.tile([P, 2], F32, name="parts", tag="parts")
            nc.scalar.activation(
                out=parts[:],
                in_=small[("sums", tau)][:],
                func=ACT.Identity,
                scale=-1.0 / D,
                accum_out=small[("nm", tau)][:],
            )

        def square(tau):
            junk = up.tile([P, D], BF16, name="junk", tag="junk", bufs=1)
            small[("ssq", tau)] = sm.tile([P, 1], F32, name="ssq", tag="ssq")
            nc.scalar.activation(
                out=junk[:],
                in_=ht[tau][:],
                func=ACT.Square,
                bias=small[("nm", tau)][:, 0:1],
                scale=1.0,
                accum_out=small[("ssq", tau)][:, 0:1],
            )

        def inverse_std(tau):
            small[("rstd", tau)] = sm.tile([P, 1], F32, name="rstd", tag="rstd")
            nc.scalar.activation(
                out=small[("rstd", tau)][:],
                in_=small[("ssq", tau)][:],
                func=ACT.Abs_reciprocal_sqrt,
                bias=eps_t[:, 0:1],
                scale=1.0 / D,
            )

        def gain(tau, nh):
            w = cols(nh)
            if tau not in ut:
                ut[tau] = up.tile([P, D], F32, name="u", tag="u")
            nc.vector.scalar_tensor_tensor(
                out=ut[tau][:, w],
                in0=ht[tau][:, w],
                scalar=small[("nm", tau)][:, 0:1],
                in1=const["og"][:, w],
                op0=ALU.add,
                op1=ALU.mult,
            )

        def diagonal(tau):
            small[("diag", tau)] = sm.tile([P, P], F32, name="diag", tag="diag", bufs=2)
            nc.gpsimd.tensor_scalar(
                out=small[("diag", tau)][:],
                in0=ident[:],
                scalar1=small[("rstd", tau)][:, 0:1],
                scalar2=0.0,
                op0=ALU.mult,
                op1=ALU.add,
            )

        def shift_pe(tau, nh):
            po = ps2.tile([P, 512], F32, name="po", tag="s2")
            acc[("sp", tau, nh)] = po
            nc.tensor.matmul(out=po[:], lhsT=mean16[:], rhs=const["be"][:, cols(nh)], start=True, stop=False)
            nc.tensor.matmul(out=po[:], lhsT=small[("diag", tau)][:], rhs=ut[tau][:, cols(nh)], start=False, stop=True)

        def shift_v(tau, nh):
            w = cols(nh)
            nc.vector.scalar_tensor_tensor(
                out=ut[tau][:, w],
                in0=ut[tau][:, w],
                scalar=small[("rstd", tau)][:, 0:1],
                in1=const["be"][:, w],
                op0=ALU.mult,
                op1=ALU.add,
            )

        def relu(tau, nh):
            w = cols(nh)
            src = acc[("sp", tau, nh)][:] if tau in PE_SHIFT else ut[tau][:, w]
            if (tau, nh) in RELU_V:
                nc.vector.tensor_scalar_max(out=ut[tau][:, w], in0=src, scalar1=0.0)
            else:
                nc.scalar.activation(out=ut[tau][:, w], in_=src, func=ACT.Relu)

        def store(tau, nh):
            b, sg = divmod(tau, 4)
            nc.sync.dma_start(out=out[b, 128 * sg : 128 * sg + 128, cols(nh)], in_=ut[tau][:, cols(nh)])
        nc.vector.memset(mean16[:], 1.0 / P)

        call = {
            "load": load, "turn": turn, "turned": turn_copy, "vs": group_v, "ss": group_s, "q": quant,
            "bc": broadcast, "s1": s1, "pack": pack, "qcb": quant_cb, "s2": s2, "a": add_ob,
            "nm": neg_mean, "dg": diagonal, "sp": shift_pe, "b": square, "rs": inverse_std, "c": gain, "d": shift_v, "e": relu, "st": store,
        }

        bank_order = [op for op in TENSOR if op[0] in ("s1", "turn")]
        acc_order = [op for op in TENSOR if op[0] in ("s2", "sp")]
        small_order = [x for b in range(2) for x in (("A", b), ("AT", b))]
        big_order = [op[1:] for op in LOADS if op[0] == "load" and op[1] != "A"]
        parts_of = {}
        for op in VECTOR + SCALAR:
            if op[0] in ("vs", "ss"):
                parts_of.setdefault(op[1:3], []).append(op)

        def ring(order, item, depth):
            k = order.index(item)
            return [order[k - depth]] if k >= depth else []

        def needs(op):
            kind, a = op[0], op[1:]
            n = []
            if kind in ("turn", "s1"):
                n += [(("pack",) if x[0] == "s1" else ("turned",)) + x[1:] for x in ring(bank_order, op, N1)]
            if kind in ("s2", "sp"):
                n += [(("a",) if x[0] == "s2" else ("e",)) + x[1:] for x in ring(acc_order, op, N2)]
            if kind == "turn":
                n += [("load", "A", a[0])]
            elif kind == "turned":
                n += [("turn",) + a] + [("q",) + x for x in ring(small_order, ("AT", a[0]), 3)]
            elif kind in ("vs", "ss"):
                n += [("load",) + a[:2]]
                n += [("q",) + x for x in (ring(small_order, a[:2], 3) if a[0] == "A" else ring(big_order, a[:2], 3))]
            elif kind == "q":
                if a[0] == "AT":
                    n += [("turned", a[1], 0), ("turned", a[1], 1)]
                else:
                    n += parts_of[a]
            elif kind == "s1":
                n += [("q", "vp" if a[1] < 2 else "lp", a[0] // 4), ("q", "AT" if a[1] < 2 else "A", a[0] // 4)]
            elif kind == "pack":
                n += [("s1",) + a] + ([("qcb", a[0] - 3)] if a[0] >= 3 else [])
            elif kind == "qcb":
                n += [("pack", a[0], g) for g in range(4)] + ([("s2", a[0] - CB, 1)] if a[0] >= CB else [])
            elif kind == "s2":
                n += [("qcb", a[0])] + [("q", "oW", g) for g in range(4)]
            elif kind == "a":
                n += [("s2",) + a, ("bc", "ob")] + ([("c", a[0] - H, -1), ("b", a[0] - H)] if a[0] >= H else [])
            elif kind == "nm":
                n += [("a", a[0], 0), ("a", a[0], 1)]
            elif kind == "b":
                n += [("nm", a[0])]
            elif kind == "rs":
                n += [("b", a[0])]
            elif kind == "c":
                n += [("nm", a[0]), ("bc", "og")] + ([("st", a[0] - U, -1)] if a[0] >= U else [])
            elif kind == "dg":
                n += [("rs", a[0])]
            elif kind == "d":
                n += [("rs", a[0]), ("c", a[0], -1), ("bc", "be")]
            elif kind == "sp":
                n += [("dg", a[0]), ("c", a[0], -1), ("bc", "be")]
            elif kind == "e":
                n += [("sp",) + a if a[0] in PE_SHIFT else ("d", a[0], -1 if a[0] < 7 else min(a[1], 1))]
            elif kind == "st":
                n += [("e",) + a] if ("e",) + a in SCALAR + VECTOR else [("e", a[0], h) for h in range(2)]
            return n

        done = set()
        queues = [list(x) for x in (LOADS, TENSOR, VECTOR, SCALAR, GPSIMD, STORES)]
        while any(queues):
            before = len(done)
            for queue in queues:
                while queue and all(x in done for x in needs(queue[0])):
                    op = queue.pop(0)
                    call[op[0]](*op[1:])
                    done.add(op)
            assert len(done) > before, [q[0] for q in queues if q]
